import numpy as np
import ml_dtypes


def mxq(x, axis, fmt="e4m3"):
    dtype, down = {"e4m3": (ml_dtypes.float8_e4m3fn, 7), "e5m2": (ml_dtypes.float8_e5m2, 14)}[fmt]
    v = np.moveaxis(np.asarray(x, np.float32).astype(ml_dtypes.bfloat16).astype(np.float64), axis, -1)
    blocks = v.reshape(v.shape[:-1] + (-1, 32))
    amax = np.abs(blocks).max(-1, keepdims=True)
    byte = np.maximum(np.where(amax > 0, np.frexp(amax)[1] - 1 + 127, 0) - down, 1)
    scale = np.exp2(byte - 127.0)
    codes = (blocks / scale).astype(np.float32).astype(dtype).astype(np.float64)
    return np.moveaxis((codes * scale).reshape(v.shape), -1, axis)


WIDE = False


def mx_kscale(k):
    if not WIDE:
        return np.ones(k)
    levels = np.array([10, -10, 5, -5, 0])
    a = np.random.permutation(np.resize(levels, k // 512 * 4)).reshape(k // 512, 4)
    idx = np.arange(k)
    return np.exp2(a[idx // 512, idx % 128 // 32])


BF16 = ml_dtypes.bfloat16


def bf(x):
    return np.asarray(x, np.float32).astype(BF16)


def f64(x):
    return np.asarray(x).astype(np.float64)


NA, NB, H = 1024, 1024, 512


def sigmoid(v):
    return 1.0 / (1.0 + np.exp(-v))


def setup_inputs():
    s, t = mx_kscale(H), mx_kscale(H)
    return {"y_a": bf(np.random.standard_normal((NA, H)) * 0.25 / t),
            "y_b": bf(np.random.standard_normal((NB, H)) * s),
            "W": bf(np.random.standard_normal((H, H)) * 6.0 / H * t[:, None] / s[None, :]),
            "b": bf(np.random.standard_normal(H) * 5.0 / np.sqrt(H) * t)}


def reference(y_a, y_b, W, b):
    proj = (mxq(f64(y_b), 1, "e4m3") @ mxq(f64(W), 1, "e4m3").T) + f64(b)
    scores = mxq(f64(y_a), 1, "e4m3") @ mxq(proj, 1, "e4m3").T
    s = np.sum(sigmoid(scores), axis=1) / y_a.shape[1]
    return np.broadcast_to(s[:, None], y_a.shape).copy()

@@ -1,0 +1,203 @@
+from contextlib import ExitStack
+
+import concourse.bass as bass
+import concourse.mybir as mybir
+import concourse.tile as tile
+from concourse.masks import make_identity
+
+F32 = mybir.dt.float32
+BF16 = mybir.dt.bfloat16
+U32 = mybir.dt.uint32
+U8 = mybir.dt.uint8
+FP8X4 = mybir.dt.float8_e4m3fn_x4
+ACT = mybir.ActivationFunctionType
+ALU = mybir.AluOpType
+
+P = 128
+NA, NB, H = 1024, 1024, 512
+FLOPS = 2 * NB * H * H + 2 * NA * NB * H
+MANUAL = False
+
+
+def tile_miscore_kernel(tc, y_a, y_b, W, b, out):
+    nc = tc.nc
+    with ExitStack() as ctx:
+        keep = ctx.enter_context(tc.tile_pool(name="keep", bufs=1))
+        outp = ctx.enter_context(tc.tile_pool(name="outp", bufs=4))
+        psum = ctx.enter_context(tc.psum_pool(name="psum", bufs=8))
+        if MANUAL:
+            ctx.enter_context(tc.manual_schedule())
+
+        w_sb = keep.tile([P, 2048], BF16, name="w_sb")
+        for u in range(2):
+            nc.sync.dma_start(
+                out=w_sb[:, 1024 * u : 1024 * (u + 1)],
+                in_=W[256 * u : 256 * (u + 1), :].rearrange("(p e) i -> p (e i)", e=2),
+            )
+        yb_sb = [keep.tile([P, 2048], BF16, name="yb_sb%d" % h) for h in range(2)]
+        ya_sb = [keep.tile([P, 2048], BF16, name="ya_sb%d" % g) for g in range(2)]
+        ya_v = y_a.rearrange("(p r) o -> p r o", r=8)
+
+        def load_yb(h):
+            nc.sync.dma_start(
+                out=yb_sb[h][:, :],
+                in_=y_b[512 * h : 512 * (h + 1), :].rearrange("(p r) i -> p (r i)", r=4),
+            )
+
+        def load_ya(g):
+            nc.sync.dma_start(
+                out=ya_sb[g][:, :].rearrange("p (r o) -> p r o", r=4),
+                in_=ya_v[:, 4 * g : 4 * (g + 1), :],
+            )
+
+        load_yb(0)
+        load_ya(0)
+        load_ya(1)
+        load_yb(1)
+
+        b_bf = keep.tile([P, 4], BF16, name="b_bf")
+        nc.scalar.dma_start(
+            out=b_bf[:, :].rearrange("p (u e) -> p u e", u=2),
+            in_=b.rearrange("(u p e) -> p u e", u=2, e=2),
+        )
+
+        warm = keep.tile([P, 1], F32, name="warm")
+        warm2 = keep.tile([P, 1], F32, name="warm2")
+        nc.vector.memset(warm[:, :], 0.0)
+        nc.scalar.activation(out=warm2[:, :], in_=warm[:, :], func=ACT.Sigmoid)
+        ident = keep.tile([P, P], F32, name="ident")
+        make_identity(nc, ident[:, :])
+        cdiv = keep.tile([P, H], F32, name="cdiv")
+        nc.vector.memset(cdiv[:, :], 1.0 / H)
+
+        def transposes(src, pair, name):
+            bank = psum.tile([P, 512], F32, name=name, tag="bank")
+            s32 = src[:, :].bitcast(F32)
+            for q in range(4):
+                c0 = 512 * pair + 128 * q
+                nc.tensor.transpose(bank[:, 128 * q : 128 * (q + 1)], s32[:, c0 : c0 + 128], ident[:, :])
+            return bank
+
+        def copy_out(eng, bank, name):
+            g = keep.tile([P, 1024], BF16, name=name, align_bytes=64)
+            dst = g[:, :].bitcast(F32).rearrange("p (r c u) -> p r c u", r=2, u=2)
+            src = bank[:, :].rearrange("p (r u c) -> p r c u", r=2, u=2)
+            if eng == "v":
+                nc.vector.tensor_copy(out=dst, in_=src)
+            else:
+                nc.scalar.copy(out=dst, in_=src)
+            return g
+
+        def quantise(g, width, name):
+            codes = keep.tile([P, width // 4], U32, name=name + "_c", align_bytes=64)
+            scales = keep.tile([P, width // 4], U8, name=name + "_s", align_bytes=64)
+            nc.vector.quantize_mx(out=codes[:, :].bitcast(FP8X4), scales=scales[:, :], in_=g[:, :])
+            return codes, scales
+
+        def cols(op, k):
+            codes, scales = op
+            return codes[:, 128 * k : 128 * (k + 1)].bitcast(FP8X4), scales[:, 128 * k : 128 * (k + 1)]
+
+        tw = [transposes(w_sb, k, "tw%d" % k) for k in range(2)]
+        gw = [copy_out("vs"[k], tw[k], "gw%d" % k) for k in range(2)]
+        tb = [transposes(yb_sb[0], k, "tb%d" % k) for k in range(2)]
+        wq = [quantise(gw[k], 1024, "wq%d" % k) for k in range(2)]
+        gb = [copy_out("vs"[k], tb[k], "gb%d" % k) for k in range(2)]
+        ta = [transposes(ya_sb[0], k, "ta%d" % k) for k in range(2)]
+        bq = [quantise(gb[k], 1024, "bq%d" % k) for k in range(2)]
+        ga = [copy_out("s", ta[k], "ga%d" % k) for k in range(2)]
+
+        bias = keep.tile([P, 4], F32, name="bias")
+        nc.vector.tensor_copy(out=bias[:, :], in_=b_bf[:, :])
+        g2 = [keep.tile([P, 2048], BF16, name="g2_%d" % h, align_bytes=64) for h in range(2)]
+        bias_b = bias[:, :].unsqueeze(1).to_broadcast([P, P, 4])
+
+        def proj_mm(jc):
+            bank = psum.tile([P, 512], F32, name="pj%d" % jc, tag="bank")
+            rhs, rhs_s = cols(bq[jc // 2], jc % 2)
+            for t in range(4):
+                lhsT, lhsT_s = cols(wq[t // 2], t % 2)
+                nc.tensor.matmul_mx(
+                    out=bank[:, 128 * t : 128 * (t + 1)],
+                    lhsT=lhsT, lhsT_scale=lhsT_s, rhs=rhs, rhs_scale=rhs_s,
+                    start=True, stop=True,
+                )
+            return bank
+
+        def proj_add(jc, bank):
+            h, k = jc // 4, jc % 4
+            nc.vector.tensor_tensor(
+                out=g2[h][:, 512 * k : 512 * (k + 1)].rearrange("p (j t) -> p j t", t=4),
+                in0=bank[:, :].rearrange("p (t j) -> p j t", t=4),
+                in1=bias_b,
+                op=ALU.add,
+            )
+
+        pj = {}
+        aq = []
+        pj[0] = proj_mm(0)
+        pj[1] = proj_mm(1)
+        proj_add(0, pj[0])
+        ta.append(transposes(ya_sb[1], 0, "ta2"))
+        ta.append(transposes(ya_sb[1], 1, "ta3"))
+        aq.append(quantise(ga[0], 1024, "aq0"))
+        proj_add(1, pj[1])
+        pj[2] = proj_mm(2)
+        pj[3] = proj_mm(3)
+        ga.append(copy_out("s", ta[2], "ga2"))
+        ga.append(copy_out("s", ta[3], "ga3"))
+        proj_add(2, pj[2])
+        aq.append(quantise(ga[1], 1024, "aq1"))
+        proj_add(3, pj[3])
+        tb.append(transposes(yb_sb[1], 0, "tb2"))
+        tb.append(transposes(yb_sb[1], 1, "tb3"))
+        gb.append(copy_out("s", tb[2], "gb2"))
+        gb.append(copy_out("s", tb[3], "gb3"))
+        pq = [None, None]
+        pq[0] = quantise(g2[0], 2048, "pq0")
+
+        acc = keep.tile([P, 16], F32, name="acc")
+        junk = keep.tile([P, 512], BF16, name="junk")
+
+        def score(h, r):
+            bank = psum.tile([P, 512], F32, name="sc%d_%d" % (h, r), tag="bank")
+            lhsT, lhsT_s = cols(aq[r // 2], r % 2)
+            nc.tensor.matmul_mx(
+                out=bank[:, :], lhsT=lhsT, lhsT_scale=lhsT_s,
+                rhs=pq[h][0][:, :].bitcast(FP8X4), rhs_scale=pq[h][1][:, :],
+                start=True, stop=True,
+            )
+            nc.scalar.activation(
+                out=junk[:, :], in_=bank[:, :], func=ACT.Sigmoid,
+                accum_out=acc[:, 8 * h + r : 8 * h + r + 1],
+            )
+
+        for r in range(4):
+            score(0, r)
+        aq.append(quantise(ga[2], 1024, "aq2"))
+        aq.append(quantise(ga[3], 1024, "aq3"))
+        bq.append(quantise(gb[2], 1024, "bq2"))
+        bq.append(quantise(gb[3], 1024, "bq3"))
+        score(0, 4)
+        score(0, 5)
+        for jc in range(4, 8):
+            pj[jc] = proj_mm(jc)
+            proj_add(jc, pj[jc])
+        pq[1] = quantise(g2[1], 2048, "pq1")
+        score(0, 6)
+        score(0, 7)
+        acc0 = keep.tile([P, 8], F32, name="acc0")
+        nc.vector.tensor_scalar(
+            out=acc0[:, :], in0=acc[:, 0:8], scalar1=1.0 / H, scalar2=None, op0=ALU.mult
+        )
+
+        out_v = out.rearrange("(p r) k -> p r k", r=8)
+        for r in range(8):
+            score(1, r)
+            o_sb = outp.tile([P, H], F32, name="o_sb")
+            nc.vector.tensor_scalar(
+                out=o_sb[:, :], in0=cdiv[:, :],
+                scalar1=acc[:, 8 + r : 9 + r], scalar2=acc0[:, r : r + 1],
+                op0=ALU.mult, op1=ALU.add,
+            )
+            nc.sync.dma_start(out=out_v[:, r, :], in_=o_sb[:, :])

@@ -16,7 +16,7 @@ ALU = mybir.AluOpType
 P = 128
 NA, NB, H = 1024, 1024, 512
 FLOPS = 2 * NB * H * H + 2 * NA * NB * H
-MANUAL = False
+MANUAL = True
 
 
 def tile_miscore_kernel(tc, y_a, y_b, W, b, out):

@@ -1,8 +1,6 @@
 from contextlib import ExitStack
 
-import concourse.bass as bass
 import concourse.mybir as mybir
-import concourse.tile as tile
 from concourse.masks import make_identity
 
 F32 = mybir.dt.float32
@@ -16,7 +14,8 @@ ALU = mybir.AluOpType
 P = 128
 NA, NB, H = 1024, 1024, 512
 FLOPS = 2 * NB * H * H + 2 * NA * NB * H
-MANUAL = True
+WIDTHS = [512, 512]
+NCH = 2
 
 
 def tile_miscore_kernel(tc, y_a, y_b, W, b, out):
@@ -24,37 +23,26 @@ def tile_miscore_kernel(tc, y_a, y_b, W, b, out):
     with ExitStack() as ctx:
         keep = ctx.enter_context(tc.tile_pool(name="keep", bufs=1))
         outp = ctx.enter_context(tc.tile_pool(name="outp", bufs=4))
-        psum = ctx.enter_context(tc.psum_pool(name="psum", bufs=8))
-        if MANUAL:
-            ctx.enter_context(tc.manual_schedule())
+        psum = ctx.enter_context(tc.psum_pool(name="psum", bufs=1))
+        ctx.enter_context(tc.manual_schedule())
 
-        w_sb = keep.tile([P, 2048], BF16, name="w_sb")
-        for u in range(2):
-            nc.sync.dma_start(
-                out=w_sb[:, 1024 * u : 1024 * (u + 1)],
-                in_=W[256 * u : 256 * (u + 1), :].rearrange("(p e) i -> p (e i)", e=2),
-            )
-        yb_sb = [keep.tile([P, 2048], BF16, name="yb_sb%d" % h) for h in range(2)]
-        ya_sb = [keep.tile([P, 2048], BF16, name="ya_sb%d" % g) for g in range(2)]
         ya_v = y_a.rearrange("(p r) o -> p r o", r=8)
-
-        def load_yb(h):
-            nc.sync.dma_start(
-                out=yb_sb[h][:, :],
-                in_=y_b[512 * h : 512 * (h + 1), :].rearrange("(p r) i -> p (r i)", r=4),
-            )
-
-        def load_ya(g):
-            nc.sync.dma_start(
-                out=ya_sb[g][:, :].rearrange("p (r o) -> p r o", r=4),
-                in_=ya_v[:, 4 * g : 4 * (g + 1), :],
-            )
-
-        load_yb(0)
-        load_ya(0)
-        load_ya(1)
-        load_yb(1)
-
+        out_v = out.rearrange("(p r) k -> p r k", r=8)
+        w0 = keep.tile([P, 1024], BF16, name="w0")
+        nc.sync.dma_start(out=w0[:, :], in_=W[0 : 256, :].rearrange("(p e) i -> p (e i)", e=2))
+        w1 = keep.tile([P, 1024], BF16, name="w1")
+        nc.sync.dma_start(out=w1[:, :], in_=W[256 : 512, :].rearrange("(p e) i -> p (e i)", e=2))
+        yb0 = keep.tile([P, 1024], BF16, name="yb0")
+        nc.sync.dma_start(out=yb0[:, :], in_=y_b[0 : 256, :].rearrange("(p r) i -> p (r i)", r=2))
+        yb1 = keep.tile([P, 1024], BF16, name="yb1")
+        nc.sync.dma_start(out=yb1[:, :], in_=y_b[256 : 512, :].rearrange("(p r) i -> p (r i)", r=2))
+        ya0 = keep.tile([P, 2048], BF16, name="ya0")
+        nc.sync.dma_start(out=ya0[:, :].rearrange("p (r o) -> p r o", r=4), in_=ya_v[:, 0 : 4, :])
+        yb2 = keep.tile([P, 2048], BF16, name="yb2")
+        nc.sync.dma_start(out=yb2[:, :], in_=y_b[512 : 1024, :].rearrange("(p r) i -> p (r i)", r=4))
+        ya1 = keep.tile([P, 2048], BF16, name="ya1")
+        nc.sync.dma_start(out=ya1[:, :].rearrange("p (r o) -> p r o", r=4), in_=ya_v[:, 4 : 8, :])
+        srcs = {"w0": (w0, 0), "w1": (w1, 0), "b0": (yb0, 0), "b1": (yb1, 0), "a0": (ya0, 0), "a1": (ya0, 1), "b2": (yb2, 0), "b3": (yb2, 1), "a2": (ya1, 0), "a3": (ya1, 1)}
         b_bf = keep.tile([P, 4], BF16, name="b_bf")
         nc.scalar.dma_start(
             out=b_bf[:, :].rearrange("p (u e) -> p u e", u=2),
@@ -69,9 +57,20 @@ def tile_miscore_kernel(tc, y_a, y_b, W, b, out):
         make_identity(nc, ident[:, :])
         cdiv = keep.tile([P, H], F32, name="cdiv")
         nc.vector.memset(cdiv[:, :], 1.0 / H)
+        bias = keep.tile([P, 4], F32, name="bias")
+        bias_b = bias[:, :].unsqueeze(1).to_broadcast([P, P, 4])
+        g2 = [keep.tile([P, 4 * WIDTHS[c]], BF16, name="g2c%d" % c, align_bytes=64) for c in range(NCH)]
+        acc = keep.tile([P, 8 * NCH], F32, name="acc")
+        acc0 = keep.tile([P, 8], F32, name="acc0")
+        junk = keep.tile([P, 512], BF16, name="junk")
+        tp, gr, qz, pj, pq, sc = {}, {}, {}, {}, {}, {}
 
-        def transposes(src, pair, name):
-            bank = psum.tile([P, 512], F32, name=name, tag="bank")
+        def bank_tile(n, name):
+            return psum.tile([P, 512], F32, name=name, tag="bank%d" % n)
+
+        def transposes(x, k, n):
+            src, pair = srcs["%s%d" % (x, k)]
+            bank = bank_tile(n, "t%s%d" % (x, k))
             s32 = src[:, :].bitcast(F32)
             for q in range(4):
                 c0 = 512 * pair + 128 * q
@@ -89,8 +88,8 @@ def tile_miscore_kernel(tc, y_a, y_b, W, b, out):
             return g
 
         def quantise(g, width, name):
-            codes = keep.tile([P, width // 4], U32, name=name + "_c", align_bytes=64)
-            scales = keep.tile([P, width // 4], U8, name=name + "_s", align_bytes=64)
+            codes = keep.tile([P, width // 4], U32, name=name + "c", align_bytes=64)
+            scales = keep.tile([P, width // 4], U8, name=name + "s", align_bytes=64)
             nc.vector.quantize_mx(out=codes[:, :].bitcast(FP8X4), scales=scales[:, :], in_=g[:, :])
             return codes, scales
 
@@ -98,25 +97,11 @@ def tile_miscore_kernel(tc, y_a, y_b, W, b, out):
             codes, scales = op
             return codes[:, 128 * k : 128 * (k + 1)].bitcast(FP8X4), scales[:, 128 * k : 128 * (k + 1)]
 
-        tw = [transposes(w_sb, k, "tw%d" % k) for k in range(2)]
-        gw = [copy_out("vs"[k], tw[k], "gw%d" % k) for k in range(2)]
-        tb = [transposes(yb_sb[0], k, "tb%d" % k) for k in range(2)]
-        wq = [quantise(gw[k], 1024, "wq%d" % k) for k in range(2)]
-        gb = [copy_out("vs"[k], tb[k], "gb%d" % k) for k in range(2)]
-        ta = [transposes(ya_sb[0], k, "ta%d" % k) for k in range(2)]
-        bq = [quantise(gb[k], 1024, "bq%d" % k) for k in range(2)]
-        ga = [copy_out("s", ta[k], "ga%d" % k) for k in range(2)]
-
-        bias = keep.tile([P, 4], F32, name="bias")
-        nc.vector.tensor_copy(out=bias[:, :], in_=b_bf[:, :])
-        g2 = [keep.tile([P, 2048], BF16, name="g2_%d" % h, align_bytes=64) for h in range(2)]
-        bias_b = bias[:, :].unsqueeze(1).to_broadcast([P, P, 4])
-
-        def proj_mm(jc):
-            bank = psum.tile([P, 512], F32, name="pj%d" % jc, tag="bank")
-            rhs, rhs_s = cols(bq[jc // 2], jc % 2)
+        def proj_mm(jc, n):
+            bank = bank_tile(n, "pj%d" % jc)
+            rhs, rhs_s = cols(qz["b%d" % (jc // 2)], jc % 2)
             for t in range(4):
-                lhsT, lhsT_s = cols(wq[t // 2], t % 2)
+                lhsT, lhsT_s = cols(qz["w%d" % (t // 2)], t % 2)
                 nc.tensor.matmul_mx(
                     out=bank[:, 128 * t : 128 * (t + 1)],
                     lhsT=lhsT, lhsT_scale=lhsT_s, rhs=rhs, rhs_scale=rhs_s,
@@ -124,80 +109,134 @@ def tile_miscore_kernel(tc, y_a, y_b, W, b, out):
                 )
             return bank
 
-        def proj_add(jc, bank):
-            h, k = jc // 4, jc % 4
+        def proj_add(bank, c, k):
             nc.vector.tensor_tensor(
-                out=g2[h][:, 512 * k : 512 * (k + 1)].rearrange("p (j t) -> p j t", t=4),
+                out=g2[c][:, 512 * k : 512 * (k + 1)].rearrange("p (j t) -> p j t", t=4),
                 in0=bank[:, :].rearrange("p (t j) -> p j t", t=4),
                 in1=bias_b,
                 op=ALU.add,
             )
 
-        pj = {}
-        aq = []
-        pj[0] = proj_mm(0)
-        pj[1] = proj_mm(1)
-        proj_add(0, pj[0])
-        ta.append(transposes(ya_sb[1], 0, "ta2"))
-        ta.append(transposes(ya_sb[1], 1, "ta3"))
-        aq.append(quantise(ga[0], 1024, "aq0"))
-        proj_add(1, pj[1])
-        pj[2] = proj_mm(2)
-        pj[3] = proj_mm(3)
-        ga.append(copy_out("s", ta[2], "ga2"))
-        ga.append(copy_out("s", ta[3], "ga3"))
-        proj_add(2, pj[2])
-        aq.append(quantise(ga[1], 1024, "aq1"))
-        proj_add(3, pj[3])
-        tb.append(transposes(yb_sb[1], 0, "tb2"))
-        tb.append(transposes(yb_sb[1], 1, "tb3"))
-        gb.append(copy_out("s", tb[2], "gb2"))
-        gb.append(copy_out("s", tb[3], "gb3"))
-        pq = [None, None]
-        pq[0] = quantise(g2[0], 2048, "pq0")
-
-        acc = keep.tile([P, 16], F32, name="acc")
-        junk = keep.tile([P, 512], BF16, name="junk")
-
-        def score(h, r):
-            bank = psum.tile([P, 512], F32, name="sc%d_%d" % (h, r), tag="bank")
-            lhsT, lhsT_s = cols(aq[r // 2], r % 2)
+        def score_mm(c, r, n):
+            bank = bank_tile(n, "sc%d_%d" % (c, r))
+            lhsT, lhsT_s = cols(qz["a%d" % (r // 2)], r % 2)
             nc.tensor.matmul_mx(
-                out=bank[:, :], lhsT=lhsT, lhsT_scale=lhsT_s,
-                rhs=pq[h][0][:, :].bitcast(FP8X4), rhs_scale=pq[h][1][:, :],
+                out=bank[:, 0 : WIDTHS[c]], lhsT=lhsT, lhsT_scale=lhsT_s,
+                rhs=pq[c][0][:, :].bitcast(FP8X4), rhs_scale=pq[c][1][:, :],
                 start=True, stop=True,
             )
+            return bank
+
+        def score_sig(c, r):
             nc.scalar.activation(
-                out=junk[:, :], in_=bank[:, :], func=ACT.Sigmoid,
-                accum_out=acc[:, 8 * h + r : 8 * h + r + 1],
+                out=junk[:, 0 : WIDTHS[c]], in_=sc[(c, r)][:, 0 : WIDTHS[c]], func=ACT.Sigmoid,
+                accum_out=acc[:, 8 * c + r : 8 * c + r + 1],
             )
 
-        for r in range(4):
-            score(0, r)
-        aq.append(quantise(ga[2], 1024, "aq2"))
-        aq.append(quantise(ga[3], 1024, "aq3"))
-        bq.append(quantise(gb[2], 1024, "bq2"))
-        bq.append(quantise(gb[3], 1024, "bq3"))
-        score(0, 4)
-        score(0, 5)
-        for jc in range(4, 8):
-            pj[jc] = proj_mm(jc)
-            proj_add(jc, pj[jc])
-        pq[1] = quantise(g2[1], 2048, "pq1")
-        score(0, 6)
-        score(0, 7)
-        acc0 = keep.tile([P, 8], F32, name="acc0")
-        nc.vector.tensor_scalar(
-            out=acc0[:, :], in0=acc[:, 0:8], scalar1=1.0 / H, scalar2=None, op0=ALU.mult
-        )
+        def early_sums():
+            if NCH == 2:
+                nc.vector.tensor_scalar(out=acc0[:, :], in0=acc[:, 0:8], scalar1=1.0 / H, scalar2=None, op0=ALU.mult)
+            else:
+                nc.vector.tensor_tensor(out=acc0[:, :], in0=acc[:, 0:8], in1=acc[:, 8:16], op=ALU.add)
+                nc.vector.tensor_scalar(out=acc0[:, :], in0=acc0[:, :], scalar1=1.0 / H, scalar2=None, op0=ALU.mult)
 
-        out_v = out.rearrange("(p r) k -> p r k", r=8)
-        for r in range(8):
-            score(1, r)
+        def finish(r):
             o_sb = outp.tile([P, H], F32, name="o_sb")
+            c = 8 * (NCH - 1) + r
             nc.vector.tensor_scalar(
                 out=o_sb[:, :], in0=cdiv[:, :],
-                scalar1=acc[:, 8 + r : 9 + r], scalar2=acc0[:, r : r + 1],
+                scalar1=acc[:, c : c + 1], scalar2=acc0[:, r : r + 1],
                 op0=ALU.mult, op1=ALU.add,
             )
             nc.sync.dma_start(out=out_v[:, r, :], in_=o_sb[:, :])
+
+        tp["w0"] = transposes("w", 0, 0)
+        tp["w1"] = transposes("w", 1, 1)
+        gr["w0"] = copy_out("s", tp["w0"], "gw0")
+        tp["b0"] = transposes("b", 0, 2)
+        gr["w1"] = copy_out("v", tp["w1"], "gw1")
+        tp["b1"] = transposes("b", 1, 3)
+        qz["w0"] = quantise(gr["w0"], 1024, "qw0")
+        gr["b0"] = copy_out("s", tp["b0"], "gb0")
+        qz["w1"] = quantise(gr["w1"], 1024, "qw1")
+        gr["b1"] = copy_out("s", tp["b1"], "gb1")
+        qz["b0"] = quantise(gr["b0"], 1024, "qb0")
+        tp["a0"] = transposes("a", 0, 4)
+        qz["b1"] = quantise(gr["b1"], 1024, "qb1")
+        pj[0] = proj_mm(0, 5)
+        gr["a0"] = copy_out("s", tp["a0"], "ga0")
+        pj[1] = proj_mm(1, 6)
+        nc.vector.tensor_copy(out=bias[:, :], in_=b_bf[:, :])
+        proj_add(pj[0], 0, 0)
+        pj[2] = proj_mm(2, 7)
+        proj_add(pj[1], 0, 1)
+        tp["b2"] = transposes("b", 2, 0)
+        qz["a0"] = quantise(gr["a0"], 1024, "qa0")
+        proj_add(pj[2], 0, 2)
+        tp["b3"] = transposes("b", 3, 1)
+        gr["b2"] = copy_out("s", tp["b2"], "gb2")
+        pj[3] = proj_mm(3, 2)
+        gr["b3"] = copy_out("s", tp["b3"], "gb3")
+        qz["b2"] = quantise(gr["b2"], 1024, "qb2")
+        tp["a1"] = transposes("a", 1, 3)
+        proj_add(pj[3], 0, 3)
+        tp["a2"] = transposes("a", 2, 4)
+        gr["a1"] = copy_out("s", tp["a1"], "ga1")
+        tp["a3"] = transposes("a", 3, 5)
+        pq[0] = quantise(g2[0], 2048, "pq0")
+        pj[4] = proj_mm(4, 6)
+        gr["a2"] = copy_out("s", tp["a2"], "ga2")
+        pj[5] = proj_mm(5, 7)
+        qz["b3"] = quantise(gr["b3"], 1024, "qb3")
+        qz["a1"] = quantise(gr["a1"], 1024, "qa1")
+        sc[(0, 0)] = score_mm(0, 0, 0)
+        gr["a3"] = copy_out("s", tp["a3"], "ga3")
+        proj_add(pj[4], 1, 0)
+        sc[(0, 1)] = score_mm(0, 1, 1)
+        sc[(0, 2)] = score_mm(0, 2, 2)
+        score_sig(0, 0)
+        qz["a2"] = quantise(gr["a2"], 1024, "qa2")
+        sc[(0, 3)] = score_mm(0, 3, 3)
+        proj_add(pj[5], 1, 1)
+        pj[6] = proj_mm(6, 4)
+        score_sig(0, 1)
+        pj[7] = proj_mm(7, 5)
+        qz["a3"] = quantise(gr["a3"], 1024, "qa3")
+        sc[(0, 4)] = score_mm(0, 4, 6)
+        score_sig(0, 2)
+        proj_add(pj[6], 1, 2)
+        sc[(0, 5)] = score_mm(0, 5, 7)
+        score_sig(0, 3)
+        sc[(0, 6)] = score_mm(0, 6, 0)
+        proj_add(pj[7], 1, 3)
+        sc[(0, 7)] = score_mm(0, 7, 1)
+        score_sig(0, 4)
+        pq[1] = quantise(g2[1], 2048, "pq1")
+        score_sig(0, 5)
+        score_sig(0, 6)
+        sc[(1, 0)] = score_mm(1, 0, 2)
+        sc[(1, 1)] = score_mm(1, 1, 3)
+        sc[(1, 2)] = score_mm(1, 2, 4)
+        score_sig(0, 7)
+        sc[(1, 3)] = score_mm(1, 3, 5)
+        sc[(1, 4)] = score_mm(1, 4, 6)
+        score_sig(1, 0)
+        early_sums()
+        sc[(1, 5)] = score_mm(1, 5, 7)
+        sc[(1, 6)] = score_mm(1, 6, 0)
+        score_sig(1, 1)
+        finish(0)
+        sc[(1, 7)] = score_mm(1, 7, 1)
+        score_sig(1, 2)
+        finish(1)
+        score_sig(1, 3)
+        finish(2)
+        score_sig(1, 4)
+        finish(3)
+        score_sig(1, 5)
+        finish(4)
+        score_sig(1, 6)
+        finish(5)
+        score_sig(1, 7)
+        finish(6)
+        finish(7)

@@ -49,6 +49,8 @@ def tile_miscore_kernel(tc, y_a, y_b, W, b, out):
             in_=b.rearrange("(u p e) -> p u e", u=2, e=2),
         )
 
+        zb = keep.tile([P, 512], BF16, name="zb")
+        nc.vector.memset(zb[:, :], 0.0)
         warm = keep.tile([P, 1], F32, name="warm")
         warm2 = keep.tile([P, 1], F32, name="warm2")
         nc.vector.memset(warm[:, :], 0.0)
@@ -64,6 +66,10 @@ def tile_miscore_kernel(tc, y_a, y_b, W, b, out):
         acc0 = keep.tile([P, 8], F32, name="acc0")
         junk = keep.tile([P, 512], BF16, name="junk")
         tp, gr, qz, pj, pq, sc = {}, {}, {}, {}, {}, {}
+        dmy = psum.tile([P, 512], F32, name="dmy", tag="bank7")
+
+        def dummy(bank):
+            nc.tensor.matmul(out=bank[:, :], lhsT=zb[:, 0:128], rhs=zb[:, :], start=True, stop=True)
 
         def bank_tile(n, name):
             return psum.tile([P, 512], F32, name=name, tag="bank%d" % n)
@@ -150,12 +156,20 @@ def tile_miscore_kernel(tc, y_a, y_b, W, b, out):
             )
             nc.sync.dma_start(out=out_v[:, r, :], in_=o_sb[:, :])
 
+        dummy(dmy)
+        dummy(dmy)
+        dummy(dmy)
+        dummy(dmy)
+        dummy(dmy)
+        dummy(dmy)
         tp["w0"] = transposes("w", 0, 0)
         tp["w1"] = transposes("w", 1, 1)
+        dummy(dmy)
         gr["w0"] = copy_out("s", tp["w0"], "gw0")
         tp["b0"] = transposes("b", 0, 2)
         gr["w1"] = copy_out("v", tp["w1"], "gw1")
         tp["b1"] = transposes("b", 1, 3)
+        dummy(dmy)
         qz["w0"] = quantise(gr["w0"], 1024, "qw0")
         gr["b0"] = copy_out("s", tp["b0"], "gb0")
         qz["w1"] = quantise(gr["w1"], 1024, "qw1")

@@ -14,8 +14,6 @@ ALU = mybir.AluOpType
 P = 128
 NA, NB, H = 1024, 1024, 512
 FLOPS = 2 * NB * H * H + 2 * NA * NB * H
-WIDTHS = [512, 512]
-NCH = 2
 
 
 def tile_miscore_kernel(tc, y_a, y_b, W, b, out):
@@ -42,7 +40,10 @@ def tile_miscore_kernel(tc, y_a, y_b, W, b, out):
         nc.sync.dma_start(out=yb2[:, :], in_=y_b[512 : 1024, :].rearrange("(p r) i -> p (r i)", r=4))
         ya1 = keep.tile([P, 2048], BF16, name="ya1")
         nc.sync.dma_start(out=ya1[:, :].rearrange("p (r o) -> p r o", r=4), in_=ya_v[:, 4 : 8, :])
-        srcs = {"w0": (w0, 0), "w1": (w1, 0), "b0": (yb0, 0), "b1": (yb1, 0), "a0": (ya0, 0), "a1": (ya0, 1), "b2": (yb2, 0), "b3": (yb2, 1), "a2": (ya1, 0), "a3": (ya1, 1)}
+        units = {"w01": (w0, 0, 2), "w2": (w1, 0, 1), "w3": (w1, 1, 1), "b0": (yb0, 0, 1), "b1": (yb0, 1, 1), "b23": (yb1, 0, 2), "b45": (yb2, 0, 2), "b67": (yb2, 2, 2), "a01": (ya0, 0, 2), "a23": (ya0, 2, 2), "a45": (ya1, 0, 2), "a67": (ya1, 2, 2)}
+        w_at = {0: ("w01", 0), 1: ("w01", 1), 2: ("w2", 0), 3: ("w3", 0)}
+        b_at = {0: ("b0", 0), 1: ("b1", 0), 2: ("b23", 0), 3: ("b23", 1), 4: ("b45", 0), 5: ("b45", 1), 6: ("b67", 0), 7: ("b67", 1)}
+        a_at = {0: ("a01", 0), 1: ("a01", 1), 2: ("a23", 0), 3: ("a23", 1), 4: ("a45", 0), 5: ("a45", 1), 6: ("a67", 0), 7: ("a67", 1)}
         b_bf = keep.tile([P, 4], BF16, name="b_bf")
         nc.scalar.dma_start(
             out=b_bf[:, :].rearrange("p (u e) -> p u e", u=2),
@@ -61,53 +62,58 @@ def tile_miscore_kernel(tc, y_a, y_b, W, b, out):
         nc.vector.memset(cdiv[:, :], 1.0 / H)
         bias = keep.tile([P, 4], F32, name="bias")
         bias_b = bias[:, :].unsqueeze(1).to_broadcast([P, P, 4])
-        g2 = [keep.tile([P, 4 * WIDTHS[c]], BF16, name="g2c%d" % c, align_bytes=64) for c in range(NCH)]
-        acc = keep.tile([P, 8 * NCH], F32, name="acc")
+        g2 = [keep.tile([P, 2048], BF16, name="g2c%d" % c, align_bytes=64) for c in range(2)]
+        pqc = [keep.tile([P, 512], U32, name="pqc%d" % c, align_bytes=64) for c in range(2)]
+        pqs = [keep.tile([P, 512], U8, name="pqs%d" % c, align_bytes=64) for c in range(2)]
+        acc = keep.tile([P, 16], F32, name="acc")
         acc0 = keep.tile([P, 8], F32, name="acc0")
         junk = keep.tile([P, 512], BF16, name="junk")
-        tp, gr, qz, pj, pq, sc = {}, {}, {}, {}, {}, {}
+        tp, gr, qz, pj, sc = {}, {}, {}, {}, {}
         dmy = psum.tile([P, 512], F32, name="dmy", tag="bank7")
 
-        def dummy(bank):
-            nc.tensor.matmul(out=bank[:, :], lhsT=zb[:, 0:128], rhs=zb[:, :], start=True, stop=True)
+        def dummy():
+            nc.tensor.matmul(out=dmy[:, :], lhsT=zb[:, 0:128], rhs=zb[:, :], start=True, stop=True)
 
         def bank_tile(n, name):
             return psum.tile([P, 512], F32, name=name, tag="bank%d" % n)
 
-        def transposes(x, k, n):
-            src, pair = srcs["%s%d" % (x, k)]
-            bank = bank_tile(n, "t%s%d" % (x, k))
+        def transposes(un, n):
+            src, off, nt = units[un]
+            bank = bank_tile(n, "t" + un)
             s32 = src[:, :].bitcast(F32)
-            for q in range(4):
-                c0 = 512 * pair + 128 * q
+            for q in range(2 * nt):
+                c0 = 256 * off + 128 * q
                 nc.tensor.transpose(bank[:, 128 * q : 128 * (q + 1)], s32[:, c0 : c0 + 128], ident[:, :])
             return bank
 
-        def copy_out(eng, bank, name):
-            g = keep.tile([P, 1024], BF16, name=name, align_bytes=64)
-            dst = g[:, :].bitcast(F32).rearrange("p (r c u) -> p r c u", r=2, u=2)
-            src = bank[:, :].rearrange("p (r u c) -> p r c u", r=2, u=2)
+        def copy_out(eng, un):
+            nt = units[un][2]
+            g = keep.tile([P, 512 * nt], BF16, name="g" + un, align_bytes=64)
+            dst = g[:, :].bitcast(F32).rearrange("p (r c u) -> p r c u", r=nt, u=2)
+            src = tp[un][:, 0 : 256 * nt].rearrange("p (r u c) -> p r c u", r=nt, u=2)
             if eng == "v":
                 nc.vector.tensor_copy(out=dst, in_=src)
             else:
                 nc.scalar.copy(out=dst, in_=src)
             return g
 
-        def quantise(g, width, name):
-            codes = keep.tile([P, width // 4], U32, name=name + "c", align_bytes=64)
-            scales = keep.tile([P, width // 4], U8, name=name + "s", align_bytes=64)
-            nc.vector.quantize_mx(out=codes[:, :].bitcast(FP8X4), scales=scales[:, :], in_=g[:, :])
+        def quantise(un):
+            nt = units[un][2]
+            codes = keep.tile([P, 128 * nt], U32, name="q" + un + "c", align_bytes=64)
+            scales = keep.tile([P, 128 * nt], U8, name="q" + un + "s", align_bytes=64)
+            nc.vector.quantize_mx(out=codes[:, :].bitcast(FP8X4), scales=scales[:, :], in_=gr[un][:, :])
             return codes, scales
 
-        def cols(op, k):
-            codes, scales = op
+        def cols(at):
+            un, k = at
+            codes, scales = qz[un]
             return codes[:, 128 * k : 128 * (k + 1)].bitcast(FP8X4), scales[:, 128 * k : 128 * (k + 1)]
 
         def proj_mm(jc, n):
             bank = bank_tile(n, "pj%d" % jc)
-            rhs, rhs_s = cols(qz["b%d" % (jc // 2)], jc % 2)
+            rhs, rhs_s = cols(b_at[jc])
             for t in range(4):
-                lhsT, lhsT_s = cols(qz["w%d" % (t // 2)], t % 2)
+                lhsT, lhsT_s = cols(w_at[t])
                 nc.tensor.matmul_mx(
                     out=bank[:, 128 * t : 128 * (t + 1)],
                     lhsT=lhsT, lhsT_scale=lhsT_s, rhs=rhs, rhs_scale=rhs_s,
@@ -123,125 +129,136 @@ def tile_miscore_kernel(tc, y_a, y_b, W, b, out):
                 op=ALU.add,
             )
 
+        def quantise_proj(c, half):
+            nc.vector.quantize_mx(
+                out=pqc[c][:, 256 * half : 256 * (half + 1)].bitcast(FP8X4),
+                scales=pqs[c][:, 256 * half : 256 * (half + 1)],
+                in_=g2[c][:, 1024 * half : 1024 * (half + 1)],
+            )
+
         def score_mm(c, r, n):
             bank = bank_tile(n, "sc%d_%d" % (c, r))
-            lhsT, lhsT_s = cols(qz["a%d" % (r // 2)], r % 2)
+            lhsT, lhsT_s = cols(a_at[r])
             nc.tensor.matmul_mx(
-                out=bank[:, 0 : WIDTHS[c]], lhsT=lhsT, lhsT_scale=lhsT_s,
-                rhs=pq[c][0][:, :].bitcast(FP8X4), rhs_scale=pq[c][1][:, :],
+                out=bank[:, :], lhsT=lhsT, lhsT_scale=lhsT_s,
+                rhs=pqc[c][:, :].bitcast(FP8X4), rhs_scale=pqs[c][:, :],
                 start=True, stop=True,
             )
             return bank
 
         def score_sig(c, r):
             nc.scalar.activation(
-                out=junk[:, 0 : WIDTHS[c]], in_=sc[(c, r)][:, 0 : WIDTHS[c]], func=ACT.Sigmoid,
+                out=junk[:, :], in_=sc[(c, r)][:, :], func=ACT.Sigmoid,
                 accum_out=acc[:, 8 * c + r : 8 * c + r + 1],
             )
 
         def early_sums():
-            if NCH == 2:
-                nc.vector.tensor_scalar(out=acc0[:, :], in0=acc[:, 0:8], scalar1=1.0 / H, scalar2=None, op0=ALU.mult)
-            else:
-                nc.vector.tensor_tensor(out=acc0[:, :], in0=acc[:, 0:8], in1=acc[:, 8:16], op=ALU.add)
-                nc.vector.tensor_scalar(out=acc0[:, :], in0=acc0[:, :], scalar1=1.0 / H, scalar2=None, op0=ALU.mult)
+            nc.vector.tensor_scalar(out=acc0[:, :], in0=acc[:, 0:8], scalar1=1.0 / H, scalar2=None, op0=ALU.mult)
 
         def finish(r):
             o_sb = outp.tile([P, H], F32, name="o_sb")
-            c = 8 * (NCH - 1) + r
             nc.vector.tensor_scalar(
                 out=o_sb[:, :], in0=cdiv[:, :],
-                scalar1=acc[:, c : c + 1], scalar2=acc0[:, r : r + 1],
+                scalar1=acc[:, 8 + r : 9 + r], scalar2=acc0[:, r : r + 1],
                 op0=ALU.mult, op1=ALU.add,
             )
             nc.sync.dma_start(out=out_v[:, r, :], in_=o_sb[:, :])
 
-        dummy(dmy)
-        dummy(dmy)
-        dummy(dmy)
-        dummy(dmy)
-        dummy(dmy)
-        dummy(dmy)
-        tp["w0"] = transposes("w", 0, 0)
-        tp["w1"] = transposes("w", 1, 1)
-        dummy(dmy)
-        gr["w0"] = copy_out("s", tp["w0"], "gw0")
-        tp["b0"] = transposes("b", 0, 2)
-        gr["w1"] = copy_out("v", tp["w1"], "gw1")
-        tp["b1"] = transposes("b", 1, 3)
-        dummy(dmy)
-        qz["w0"] = quantise(gr["w0"], 1024, "qw0")
-        gr["b0"] = copy_out("s", tp["b0"], "gb0")
-        qz["w1"] = quantise(gr["w1"], 1024, "qw1")
-        gr["b1"] = copy_out("s", tp["b1"], "gb1")
-        qz["b0"] = quantise(gr["b0"], 1024, "qb0")
-        tp["a0"] = transposes("a", 0, 4)
-        qz["b1"] = quantise(gr["b1"], 1024, "qb1")
-        pj[0] = proj_mm(0, 5)
-        gr["a0"] = copy_out("s", tp["a0"], "ga0")
-        pj[1] = proj_mm(1, 6)
+        dummy()
+        dummy()
+        dummy()
+        dummy()
+        dummy()
+        dummy()
+        tp["w01"] = transposes("w01", 0)
+        tp["w2"] = transposes("w2", 1)
+        gr["w01"] = copy_out("s", "w01")
+        tp["w3"] = transposes("w3", 2)
+        dummy()
+        gr["w2"] = copy_out("v", "w2")
+        tp["b0"] = transposes("b0", 3)
+        gr["w3"] = copy_out("s", "w3")
+        tp["b1"] = transposes("b1", 4)
+        qz["w01"] = quantise("w01")
+        gr["b0"] = copy_out("s", "b0")
+        qz["w2"] = quantise("w2")
+        tp["b23"] = transposes("b23", 5)
+        dummy()
+        dummy()
+        qz["w3"] = quantise("w3")
+        gr["b1"] = copy_out("s", "b1")
+        qz["b0"] = quantise("b0")
+        gr["b23"] = copy_out("s", "b23")
+        qz["b1"] = quantise("b1")
+        pj[0] = proj_mm(0, 6)
+        pj[1] = proj_mm(1, 7)
+        qz["b23"] = quantise("b23")
         nc.vector.tensor_copy(out=bias[:, :], in_=b_bf[:, :])
         proj_add(pj[0], 0, 0)
-        pj[2] = proj_mm(2, 7)
+        tp["a01"] = transposes("a01", 0)
+        tp["a23"] = transposes("a23", 1)
         proj_add(pj[1], 0, 1)
-        tp["b2"] = transposes("b", 2, 0)
-        qz["a0"] = quantise(gr["a0"], 1024, "qa0")
+        gr["a01"] = copy_out("s", "a01")
+        pj[2] = proj_mm(2, 2)
+        pj[3] = proj_mm(3, 3)
+        quantise_proj(0, 0)
+        gr["a23"] = copy_out("s", "a23")
         proj_add(pj[2], 0, 2)
-        tp["b3"] = transposes("b", 3, 1)
-        gr["b2"] = copy_out("s", tp["b2"], "gb2")
-        pj[3] = proj_mm(3, 2)
-        gr["b3"] = copy_out("s", tp["b3"], "gb3")
-        qz["b2"] = quantise(gr["b2"], 1024, "qb2")
-        tp["a1"] = transposes("a", 1, 3)
+        tp["b45"] = transposes("b45", 4)
+        tp["b67"] = transposes("b67", 5)
         proj_add(pj[3], 0, 3)
-        tp["a2"] = transposes("a", 2, 4)
-        gr["a1"] = copy_out("s", tp["a1"], "ga1")
-        tp["a3"] = transposes("a", 3, 5)
-        pq[0] = quantise(g2[0], 2048, "pq0")
-        pj[4] = proj_mm(4, 6)
-        gr["a2"] = copy_out("s", tp["a2"], "ga2")
-        pj[5] = proj_mm(5, 7)
-        qz["b3"] = quantise(gr["b3"], 1024, "qb3")
-        qz["a1"] = quantise(gr["a1"], 1024, "qa1")
+        gr["b45"] = copy_out("s", "b45")
+        tp["a45"] = transposes("a45", 6)
+        tp["a67"] = transposes("a67", 7)
+        qz["a01"] = quantise("a01")
+        gr["b67"] = copy_out("s", "b67")
+        quantise_proj(0, 1)
+        qz["a23"] = quantise("a23")
+        gr["a45"] = copy_out("s", "a45")
+        qz["b45"] = quantise("b45")
         sc[(0, 0)] = score_mm(0, 0, 0)
-        gr["a3"] = copy_out("s", tp["a3"], "ga3")
-        proj_add(pj[4], 1, 0)
+        qz["b67"] = quantise("b67")
         sc[(0, 1)] = score_mm(0, 1, 1)
-        sc[(0, 2)] = score_mm(0, 2, 2)
+        gr["a67"] = copy_out("v", "a67")
+        pj[4] = proj_mm(4, 2)
         score_sig(0, 0)
-        qz["a2"] = quantise(gr["a2"], 1024, "qa2")
-        sc[(0, 3)] = score_mm(0, 3, 3)
-        proj_add(pj[5], 1, 1)
-        pj[6] = proj_mm(6, 4)
+        pj[5] = proj_mm(5, 3)
+        sc[(0, 2)] = score_mm(0, 2, 4)
+        proj_add(pj[4], 1, 0)
         score_sig(0, 1)
-        pj[7] = proj_mm(7, 5)
-        qz["a3"] = quantise(gr["a3"], 1024, "qa3")
-        sc[(0, 4)] = score_mm(0, 4, 6)
+        sc[(0, 3)] = score_mm(0, 3, 5)
+        pj[6] = proj_mm(6, 6)
+        qz["a45"] = quantise("a45")
         score_sig(0, 2)
-        proj_add(pj[6], 1, 2)
-        sc[(0, 5)] = score_mm(0, 5, 7)
+        pj[7] = proj_mm(7, 7)
+        proj_add(pj[5], 1, 1)
+        sc[(0, 4)] = score_mm(0, 4, 0)
         score_sig(0, 3)
-        sc[(0, 6)] = score_mm(0, 6, 0)
-        proj_add(pj[7], 1, 3)
-        sc[(0, 7)] = score_mm(0, 7, 1)
+        quantise_proj(1, 0)
+        sc[(0, 5)] = score_mm(0, 5, 1)
+        qz["a67"] = quantise("a67")
         score_sig(0, 4)
-        pq[1] = quantise(g2[1], 2048, "pq1")
+        proj_add(pj[6], 1, 2)
+        sc[(0, 6)] = score_mm(0, 6, 2)
         score_sig(0, 5)
+        proj_add(pj[7], 1, 3)
+        sc[(0, 7)] = score_mm(0, 7, 3)
         score_sig(0, 6)
-        sc[(1, 0)] = score_mm(1, 0, 2)
-        sc[(1, 1)] = score_mm(1, 1, 3)
-        sc[(1, 2)] = score_mm(1, 2, 4)
+        quantise_proj(1, 1)
         score_sig(0, 7)
-        sc[(1, 3)] = score_mm(1, 3, 5)
-        sc[(1, 4)] = score_mm(1, 4, 6)
+        sc[(1, 0)] = score_mm(1, 0, 4)
+        sc[(1, 1)] = score_mm(1, 1, 5)
+        sc[(1, 2)] = score_mm(1, 2, 6)
         score_sig(1, 0)
         early_sums()
-        sc[(1, 5)] = score_mm(1, 5, 7)
-        sc[(1, 6)] = score_mm(1, 6, 0)
+        sc[(1, 3)] = score_mm(1, 3, 7)
+        sc[(1, 4)] = score_mm(1, 4, 0)
         score_sig(1, 1)
         finish(0)
-        sc[(1, 7)] = score_mm(1, 7, 1)
+        sc[(1, 5)] = score_mm(1, 5, 1)
+        sc[(1, 6)] = score_mm(1, 6, 2)
         score_sig(1, 2)
+        sc[(1, 7)] = score_mm(1, 7, 3)
         finish(1)
         score_sig(1, 3)
         finish(2)

@@ -14,6 +14,8 @@ ALU = mybir.AluOpType
 P = 128
 NA, NB, H = 1024, 1024, 512
 FLOPS = 2 * NB * H * H + 2 * NA * NB * H
+WIDTHS = [512, 512]
+NCH = 2
 
 
 def tile_miscore_kernel(tc, y_a, y_b, W, b, out):
@@ -40,18 +42,15 @@ def tile_miscore_kernel(tc, y_a, y_b, W, b, out):
         nc.sync.dma_start(out=yb2[:, :], in_=y_b[512 : 1024, :].rearrange("(p r) i -> p (r i)", r=4))
         ya1 = keep.tile([P, 2048], BF16, name="ya1")
         nc.sync.dma_start(out=ya1[:, :].rearrange("p (r o) -> p r o", r=4), in_=ya_v[:, 4 : 8, :])
-        units = {"w01": (w0, 0, 2), "w2": (w1, 0, 1), "w3": (w1, 1, 1), "b0": (yb0, 0, 1), "b1": (yb0, 1, 1), "b23": (yb1, 0, 2), "b45": (yb2, 0, 2), "b67": (yb2, 2, 2), "a01": (ya0, 0, 2), "a23": (ya0, 2, 2), "a45": (ya1, 0, 2), "a67": (ya1, 2, 2)}
-        w_at = {0: ("w01", 0), 1: ("w01", 1), 2: ("w2", 0), 3: ("w3", 0)}
-        b_at = {0: ("b0", 0), 1: ("b1", 0), 2: ("b23", 0), 3: ("b23", 1), 4: ("b45", 0), 5: ("b45", 1), 6: ("b67", 0), 7: ("b67", 1)}
-        a_at = {0: ("a01", 0), 1: ("a01", 1), 2: ("a23", 0), 3: ("a23", 1), 4: ("a45", 0), 5: ("a45", 1), 6: ("a67", 0), 7: ("a67", 1)}
+        srcs = {"w0": (w0, 0), "w1": (w1, 0), "b0": (yb0, 0), "b1": (yb1, 0), "a0": (ya0, 0), "a1": (ya0, 1), "b2": (yb2, 0), "b3": (yb2, 1), "a2": (ya1, 0), "a3": (ya1, 1)}
         b_bf = keep.tile([P, 4], BF16, name="b_bf")
         nc.scalar.dma_start(
             out=b_bf[:, :].rearrange("p (u e) -> p u e", u=2),
             in_=b.rearrange("(u p e) -> p u e", u=2, e=2),
         )
 
-        zb = keep.tile([P, 512], BF16, name="zb")
-        nc.vector.memset(zb[:, :], 0.0)
+        zf = keep.tile([P, P], F32, name="zf")
+        nc.vector.memset(zf[:, :], 0.0)
         warm = keep.tile([P, 1], F32, name="warm")
         warm2 = keep.tile([P, 1], F32, name="warm2")
         nc.vector.memset(warm[:, :], 0.0)
@@ -62,58 +61,53 @@ def tile_miscore_kernel(tc, y_a, y_b, W, b, out):
         nc.vector.memset(cdiv[:, :], 1.0 / H)
         bias = keep.tile([P, 4], F32, name="bias")
         bias_b = bias[:, :].unsqueeze(1).to_broadcast([P, P, 4])
-        g2 = [keep.tile([P, 2048], BF16, name="g2c%d" % c, align_bytes=64) for c in range(2)]
-        pqc = [keep.tile([P, 512], U32, name="pqc%d" % c, align_bytes=64) for c in range(2)]
-        pqs = [keep.tile([P, 512], U8, name="pqs%d" % c, align_bytes=64) for c in range(2)]
-        acc = keep.tile([P, 16], F32, name="acc")
+        g2 = [keep.tile([P, 4 * WIDTHS[c]], BF16, name="g2c%d" % c, align_bytes=64) for c in range(NCH)]
+        acc = keep.tile([P, 8 * NCH], F32, name="acc")
         acc0 = keep.tile([P, 8], F32, name="acc0")
         junk = keep.tile([P, 512], BF16, name="junk")
-        tp, gr, qz, pj, sc = {}, {}, {}, {}, {}
+        tp, gr, qz, pj, pq, sc = {}, {}, {}, {}, {}, {}
         dmy = psum.tile([P, 512], F32, name="dmy", tag="bank7")
 
-        def dummy():
-            nc.tensor.matmul(out=dmy[:, :], lhsT=zb[:, 0:128], rhs=zb[:, :], start=True, stop=True)
+        def dummy(bank):
+            nc.tensor.matmul(out=bank[:, 0:P], lhsT=zf[:, :], rhs=zf[:, :], start=True, stop=True)
 
         def bank_tile(n, name):
             return psum.tile([P, 512], F32, name=name, tag="bank%d" % n)
 
-        def transposes(un, n):
-            src, off, nt = units[un]
-            bank = bank_tile(n, "t" + un)
+        def transposes(x, k, n):
+            src, pair = srcs["%s%d" % (x, k)]
+            bank = bank_tile(n, "t%s%d" % (x, k))
             s32 = src[:, :].bitcast(F32)
-            for q in range(2 * nt):
-                c0 = 256 * off + 128 * q
+            for q in range(4):
+                c0 = 512 * pair + 128 * q
                 nc.tensor.transpose(bank[:, 128 * q : 128 * (q + 1)], s32[:, c0 : c0 + 128], ident[:, :])
             return bank
 
-        def copy_out(eng, un):
-            nt = units[un][2]
-            g = keep.tile([P, 512 * nt], BF16, name="g" + un, align_bytes=64)
-            dst = g[:, :].bitcast(F32).rearrange("p (r c u) -> p r c u", r=nt, u=2)
-            src = tp[un][:, 0 : 256 * nt].rearrange("p (r u c) -> p r c u", r=nt, u=2)
+        def copy_out(eng, bank, name):
+            g = keep.tile([P, 1024], BF16, name=name, align_bytes=64)
+            dst = g[:, :].bitcast(F32).rearrange("p (r c u) -> p r c u", r=2, u=2)
+            src = bank[:, :].rearrange("p (r u c) -> p r c u", r=2, u=2)
             if eng == "v":
                 nc.vector.tensor_copy(out=dst, in_=src)
             else:
                 nc.scalar.copy(out=dst, in_=src)
             return g
 
-        def quantise(un):
-            nt = units[un][2]
-            codes = keep.tile([P, 128 * nt], U32, name="q" + un + "c", align_bytes=64)
-            scales = keep.tile([P, 128 * nt], U8, name="q" + un + "s", align_bytes=64)
-            nc.vector.quantize_mx(out=codes[:, :].bitcast(FP8X4), scales=scales[:, :], in_=gr[un][:, :])
+        def quantise(g, width, name):
+            codes = keep.tile([P, width // 4], U32, name=name + "c", align_bytes=64)
+            scales = keep.tile([P, width // 4], U8, name=name + "s", align_bytes=64)
+            nc.vector.quantize_mx(out=codes[:, :].bitcast(FP8X4), scales=scales[:, :], in_=g[:, :])
             return codes, scales
 
-        def cols(at):
-            un, k = at
-            codes, scales = qz[un]
+        def cols(op, k):
+            codes, scales = op
             return codes[:, 128 * k : 128 * (k + 1)].bitcast(FP8X4), scales[:, 128 * k : 128 * (k + 1)]
 
         def proj_mm(jc, n):
             bank = bank_tile(n, "pj%d" % jc)
-            rhs, rhs_s = cols(b_at[jc])
+            rhs, rhs_s = cols(qz["b%d" % (jc // 2)], jc % 2)
             for t in range(4):
-                lhsT, lhsT_s = cols(w_at[t])
+                lhsT, lhsT_s = cols(qz["w%d" % (t // 2)], t % 2)
                 nc.tensor.matmul_mx(
                     out=bank[:, 128 * t : 128 * (t + 1)],
                     lhsT=lhsT, lhsT_scale=lhsT_s, rhs=rhs, rhs_scale=rhs_s,
@@ -129,136 +123,133 @@ def tile_miscore_kernel(tc, y_a, y_b, W, b, out):
                 op=ALU.add,
             )
 
-        def quantise_proj(c, half):
-            nc.vector.quantize_mx(
-                out=pqc[c][:, 256 * half : 256 * (half + 1)].bitcast(FP8X4),
-                scales=pqs[c][:, 256 * half : 256 * (half + 1)],
-                in_=g2[c][:, 1024 * half : 1024 * (half + 1)],
-            )
-
         def score_mm(c, r, n):
             bank = bank_tile(n, "sc%d_%d" % (c, r))
-            lhsT, lhsT_s = cols(a_at[r])
+            lhsT, lhsT_s = cols(qz["a%d" % (r // 2)], r % 2)
             nc.tensor.matmul_mx(
-                out=bank[:, :], lhsT=lhsT, lhsT_scale=lhsT_s,
-                rhs=pqc[c][:, :].bitcast(FP8X4), rhs_scale=pqs[c][:, :],
+                out=bank[:, 0 : WIDTHS[c]], lhsT=lhsT, lhsT_scale=lhsT_s,
+                rhs=pq[c][0][:, :].bitcast(FP8X4), rhs_scale=pq[c][1][:, :],
                 start=True, stop=True,
             )
             return bank
 
         def score_sig(c, r):
             nc.scalar.activation(
-                out=junk[:, :], in_=sc[(c, r)][:, :], func=ACT.Sigmoid,
+                out=junk[:, 0 : WIDTHS[c]], in_=sc[(c, r)][:, 0 : WIDTHS[c]], func=ACT.Sigmoid,
                 accum_out=acc[:, 8 * c + r : 8 * c + r + 1],
             )
 
         def early_sums():
-            nc.vector.tensor_scalar(out=acc0[:, :], in0=acc[:, 0:8], scalar1=1.0 / H, scalar2=None, op0=ALU.mult)
+            if NCH == 2:
+                nc.vector.tensor_scalar(out=acc0[:, :], in0=acc[:, 0:8], scalar1=1.0 / H, scalar2=None, op0=ALU.mult)
+            else:
+                nc.vector.tensor_tensor(out=acc0[:, :], in0=acc[:, 0:8], in1=acc[:, 8:16], op=ALU.add)
+                nc.vector.tensor_scalar(out=acc0[:, :], in0=acc0[:, :], scalar1=1.0 / H, scalar2=None, op0=ALU.mult)
 
         def finish(r):
             o_sb = outp.tile([P, H], F32, name="o_sb")
+            c = 8 * (NCH - 1) + r
             nc.vector.tensor_scalar(
                 out=o_sb[:, :], in0=cdiv[:, :],
-                scalar1=acc[:, 8 + r : 9 + r], scalar2=acc0[:, r : r + 1],
+                scalar1=acc[:, c : c + 1], scalar2=acc0[:, r : r + 1],
                 op0=ALU.mult, op1=ALU.add,
             )
             nc.sync.dma_start(out=out_v[:, r, :], in_=o_sb[:, :])
 
-        dummy()
-        dummy()
-        dummy()
-        dummy()
-        dummy()
-        dummy()
-        tp["w01"] = transposes("w01", 0)
-        tp["w2"] = transposes("w2", 1)
-        gr["w01"] = copy_out("s", "w01")
-        tp["w3"] = transposes("w3", 2)
-        dummy()
-        gr["w2"] = copy_out("v", "w2")
-        tp["b0"] = transposes("b0", 3)
-        gr["w3"] = copy_out("s", "w3")
-        tp["b1"] = transposes("b1", 4)
-        qz["w01"] = quantise("w01")
-        gr["b0"] = copy_out("s", "b0")
-        qz["w2"] = quantise("w2")
-        tp["b23"] = transposes("b23", 5)
-        dummy()
-        dummy()
-        qz["w3"] = quantise("w3")
-        gr["b1"] = copy_out("s", "b1")
-        qz["b0"] = quantise("b0")
-        gr["b23"] = copy_out("s", "b23")
-        qz["b1"] = quantise("b1")
-        pj[0] = proj_mm(0, 6)
-        pj[1] = proj_mm(1, 7)
-        qz["b23"] = quantise("b23")
+        dummy(dmy)
+        dummy(dmy)
+        dummy(dmy)
+        dummy(dmy)
+        dummy(dmy)
+        dummy(dmy)
+        tp["w0"] = transposes("w", 0, 0)
+        dummy(dmy)
+        tp["w1"] = transposes("w", 1, 1)
+        dummy(dmy)
+        gr["w0"] = copy_out("s", tp["w0"], "gw0")
+        tp["b0"] = transposes("b", 0, 2)
+        dummy(dmy)
+        gr["w1"] = copy_out("v", tp["w1"], "gw1")
+        tp["b1"] = transposes("b", 1, 3)
+        dummy(dmy)
+        dummy(dmy)
+        dummy(dmy)
+        qz["w0"] = quantise(gr["w0"], 1024, "qw0")
+        gr["b0"] = copy_out("s", tp["b0"], "gb0")
+        qz["w1"] = quantise(gr["w1"], 1024, "qw1")
+        gr["b1"] = copy_out("s", tp["b1"], "gb1")
+        qz["b0"] = quantise(gr["b0"], 1024, "qb0")
+        tp["a0"] = transposes("a", 0, 4)
+        qz["b1"] = quantise(gr["b1"], 1024, "qb1")
+        pj[0] = proj_mm(0, 5)
+        gr["a0"] = copy_out("s", tp["a0"], "ga0")
+        pj[1] = proj_mm(1, 6)
         nc.vector.tensor_copy(out=bias[:, :], in_=b_bf[:, :])
         proj_add(pj[0], 0, 0)
-        tp["a01"] = transposes("a01", 0)
-        tp["a23"] = transposes("a23", 1)
+        pj[2] = proj_mm(2, 7)
         proj_add(pj[1], 0, 1)
-        gr["a01"] = copy_out("s", "a01")
-        pj[2] = proj_mm(2, 2)
-        pj[3] = proj_mm(3, 3)
-        quantise_proj(0, 0)
-        gr["a23"] = copy_out("s", "a23")
+        tp["b2"] = transposes("b", 2, 0)
+        qz["a0"] = quantise(gr["a0"], 1024, "qa0")
         proj_add(pj[2], 0, 2)
-        tp["b45"] = transposes("b45", 4)
-        tp["b67"] = transposes("b67", 5)
+        tp["b3"] = transposes("b", 3, 1)
+        late = bank_tile(2, "late0")
+        dummy(late)
+        gr["b2"] = copy_out("s", tp["b2"], "gb2")
+        pj[3] = proj_mm(3, 3)
+        gr["b3"] = copy_out("s", tp["b3"], "gb3")
+        qz["b2"] = quantise(gr["b2"], 1024, "qb2")
+        tp["a1"] = transposes("a", 1, 4)
         proj_add(pj[3], 0, 3)
-        gr["b45"] = copy_out("s", "b45")
-        tp["a45"] = transposes("a45", 6)
-        tp["a67"] = transposes("a67", 7)
-        qz["a01"] = quantise("a01")
-        gr["b67"] = copy_out("s", "b67")
-        quantise_proj(0, 1)
-        qz["a23"] = quantise("a23")
-        gr["a45"] = copy_out("s", "a45")
-        qz["b45"] = quantise("b45")
-        sc[(0, 0)] = score_mm(0, 0, 0)
-        qz["b67"] = quantise("b67")
-        sc[(0, 1)] = score_mm(0, 1, 1)
-        gr["a67"] = copy_out("v", "a67")
-        pj[4] = proj_mm(4, 2)
-        score_sig(0, 0)
-        pj[5] = proj_mm(5, 3)
-        sc[(0, 2)] = score_mm(0, 2, 4)
+        tp["a2"] = transposes("a", 2, 5)
+        gr["a1"] = copy_out("s", tp["a1"], "ga1")
+        tp["a3"] = transposes("a", 3, 6)
+        late = bank_tile(7, "late1")
+        dummy(late)
+        pq[0] = quantise(g2[0], 2048, "pq0")
+        pj[4] = proj_mm(4, 0)
+        gr["a2"] = copy_out("s", tp["a2"], "ga2")
+        pj[5] = proj_mm(5, 1)
+        qz["b3"] = quantise(gr["b3"], 1024, "qb3")
+        qz["a1"] = quantise(gr["a1"], 1024, "qa1")
+        sc[(0, 0)] = score_mm(0, 0, 2)
+        gr["a3"] = copy_out("s", tp["a3"], "ga3")
         proj_add(pj[4], 1, 0)
-        score_sig(0, 1)
+        sc[(0, 1)] = score_mm(0, 1, 3)
+        sc[(0, 2)] = score_mm(0, 2, 4)
+        score_sig(0, 0)
+        qz["a2"] = quantise(gr["a2"], 1024, "qa2")
         sc[(0, 3)] = score_mm(0, 3, 5)
-        pj[6] = proj_mm(6, 6)
-        qz["a45"] = quantise("a45")
-        score_sig(0, 2)
-        pj[7] = proj_mm(7, 7)
         proj_add(pj[5], 1, 1)
+        pj[6] = proj_mm(6, 6)
+        score_sig(0, 1)
+        pj[7] = proj_mm(7, 7)
+        qz["a3"] = quantise(gr["a3"], 1024, "qa3")
         sc[(0, 4)] = score_mm(0, 4, 0)
-        score_sig(0, 3)
-        quantise_proj(1, 0)
-        sc[(0, 5)] = score_mm(0, 5, 1)
-        qz["a67"] = quantise("a67")
-        score_sig(0, 4)
+        score_sig(0, 2)
         proj_add(pj[6], 1, 2)
+        sc[(0, 5)] = score_mm(0, 5, 1)
+        score_sig(0, 3)
         sc[(0, 6)] = score_mm(0, 6, 2)
-        score_sig(0, 5)
         proj_add(pj[7], 1, 3)
         sc[(0, 7)] = score_mm(0, 7, 3)
+        score_sig(0, 4)
+        pq[1] = quantise(g2[1], 2048, "pq1")
+        score_sig(0, 5)
         score_sig(0, 6)
-        quantise_proj(1, 1)
-        score_sig(0, 7)
         sc[(1, 0)] = score_mm(1, 0, 4)
         sc[(1, 1)] = score_mm(1, 1, 5)
         sc[(1, 2)] = score_mm(1, 2, 6)
-        score_sig(1, 0)
-        early_sums()
+        score_sig(0, 7)
         sc[(1, 3)] = score_mm(1, 3, 7)
         sc[(1, 4)] = score_mm(1, 4, 0)
-        score_sig(1, 1)
-        finish(0)
+        score_sig(1, 0)
+        early_sums()
         sc[(1, 5)] = score_mm(1, 5, 1)
         sc[(1, 6)] = score_mm(1, 6, 2)
-        score_sig(1, 2)
+        score_sig(1, 1)
+        finish(0)
         sc[(1, 7)] = score_mm(1, 7, 3)
+        score_sig(1, 2)
         finish(1)
         score_sig(1, 3)
         finish(2)

@@ -14,251 +14,217 @@ ALU = mybir.AluOpType
 P = 128
 NA, NB, H = 1024, 1024, 512
 FLOPS = 2 * NB * H * H + 2 * NA * NB * H
-WIDTHS = [512, 512]
-NCH = 2
+PACK = 4
+BANK = 512
+N_BANKS = 8
+ROW_TILES = NA // P
+J_HALF = NB // 2
+IDLE_FIRST = 6
 
 
 def tile_miscore_kernel(tc, y_a, y_b, W, b, out):
     nc = tc.nc
     with ExitStack() as ctx:
         keep = ctx.enter_context(tc.tile_pool(name="keep", bufs=1))
-        outp = ctx.enter_context(tc.tile_pool(name="outp", bufs=4))
+        results = ctx.enter_context(tc.tile_pool(name="results", bufs=4))
         psum = ctx.enter_context(tc.psum_pool(name="psum", bufs=1))
         ctx.enter_context(tc.manual_schedule())
 
-        ya_v = y_a.rearrange("(p r) o -> p r o", r=8)
-        out_v = out.rearrange("(p r) k -> p r k", r=8)
-        w0 = keep.tile([P, 1024], BF16, name="w0")
-        nc.sync.dma_start(out=w0[:, :], in_=W[0 : 256, :].rearrange("(p e) i -> p (e i)", e=2))
-        w1 = keep.tile([P, 1024], BF16, name="w1")
-        nc.sync.dma_start(out=w1[:, :], in_=W[256 : 512, :].rearrange("(p e) i -> p (e i)", e=2))
-        yb0 = keep.tile([P, 1024], BF16, name="yb0")
-        nc.sync.dma_start(out=yb0[:, :], in_=y_b[0 : 256, :].rearrange("(p r) i -> p (r i)", r=2))
-        yb1 = keep.tile([P, 1024], BF16, name="yb1")
-        nc.sync.dma_start(out=yb1[:, :], in_=y_b[256 : 512, :].rearrange("(p r) i -> p (r i)", r=2))
-        ya0 = keep.tile([P, 2048], BF16, name="ya0")
-        nc.sync.dma_start(out=ya0[:, :].rearrange("p (r o) -> p r o", r=4), in_=ya_v[:, 0 : 4, :])
-        yb2 = keep.tile([P, 2048], BF16, name="yb2")
-        nc.sync.dma_start(out=yb2[:, :], in_=y_b[512 : 1024, :].rearrange("(p r) i -> p (r i)", r=4))
-        ya1 = keep.tile([P, 2048], BF16, name="ya1")
-        nc.sync.dma_start(out=ya1[:, :].rearrange("p (r o) -> p r o", r=4), in_=ya_v[:, 4 : 8, :])
-        srcs = {"w0": (w0, 0), "w1": (w1, 0), "b0": (yb0, 0), "b1": (yb1, 0), "a0": (ya0, 0), "a1": (ya0, 1), "b2": (yb2, 0), "b3": (yb2, 1), "a2": (ya1, 0), "a3": (ya1, 1)}
-        b_bf = keep.tile([P, 4], BF16, name="b_bf")
+        def load(name, n_tiles, rows):
+            t = keep.tile([P, n_tiles * H], BF16, name=name)
+            nc.sync.dma_start(out=t[:, :].rearrange("p (r k) -> p r k", r=n_tiles), in_=rows)
+            return t
+
+        ya_rows = y_a.rearrange("(p r) k -> p r k", r=ROW_TILES)
+        out_rows = out.rearrange("(p r) k -> p r k", r=ROW_TILES)
+        w_lo = load("w_lo", 2, W[0:256, :].rearrange("(p e) k -> p e k", e=2))
+        w_hi = load("w_hi", 2, W[256:512, :].rearrange("(p e) k -> p e k", e=2))
+        yb_0 = load("yb_0", 2, y_b[0:256, :].rearrange("(p r) k -> p r k", r=2))
+        yb_1 = load("yb_1", 2, y_b[256:512, :].rearrange("(p r) k -> p r k", r=2))
+        ya_lo = load("ya_lo", 4, ya_rows[:, 0:4, :])
+        yb_hi = load("yb_hi", 4, y_b[512:1024, :].rearrange("(p r) k -> p r k", r=4))
+        ya_hi = load("ya_hi", 4, ya_rows[:, 4:8, :])
+        source = {
+            "w0": (w_lo, 0), "w1": (w_hi, 0),
+            "b0": (yb_0, 0), "b1": (yb_1, 0), "b2": (yb_hi, 0), "b3": (yb_hi, 1),
+            "a0": (ya_lo, 0), "a1": (ya_lo, 1), "a2": (ya_hi, 0), "a3": (ya_hi, 1),
+        }
+        b_bf = keep.tile([P, PACK], BF16, name="b_bf")
         nc.scalar.dma_start(
             out=b_bf[:, :].rearrange("p (u e) -> p u e", u=2),
             in_=b.rearrange("(u p e) -> p u e", u=2, e=2),
         )
 
-        zf = keep.tile([P, P], F32, name="zf")
-        nc.vector.memset(zf[:, :], 0.0)
-        warm = keep.tile([P, 1], F32, name="warm")
-        warm2 = keep.tile([P, 1], F32, name="warm2")
-        nc.vector.memset(warm[:, :], 0.0)
-        nc.scalar.activation(out=warm2[:, :], in_=warm[:, :], func=ACT.Sigmoid)
+        zeros = keep.tile([P, BANK], BF16, name="zeros")
+        nc.vector.memset(zeros[:, :], 0.0)
+        one_col = keep.tile([P, 1], F32, name="one_col")
+        one_sig = keep.tile([P, 1], F32, name="one_sig")
+        nc.vector.memset(one_col[:, :], 0.0)
+        nc.scalar.activation(out=one_sig[:, :], in_=one_col[:, :], func=ACT.Sigmoid)
         ident = keep.tile([P, P], F32, name="ident")
         make_identity(nc, ident[:, :])
-        cdiv = keep.tile([P, H], F32, name="cdiv")
-        nc.vector.memset(cdiv[:, :], 1.0 / H)
-        bias = keep.tile([P, 4], F32, name="bias")
-        bias_b = bias[:, :].unsqueeze(1).to_broadcast([P, P, 4])
-        g2 = [keep.tile([P, 4 * WIDTHS[c]], BF16, name="g2c%d" % c, align_bytes=64) for c in range(NCH)]
-        acc = keep.tile([P, 8 * NCH], F32, name="acc")
-        acc0 = keep.tile([P, 8], F32, name="acc0")
-        junk = keep.tile([P, 512], BF16, name="junk")
-        tp, gr, qz, pj, pq, sc = {}, {}, {}, {}, {}, {}
-        dmy = psum.tile([P, 512], F32, name="dmy", tag="bank7")
+        inv_h = keep.tile([P, H], F32, name="inv_h")
+        nc.vector.memset(inv_h[:, :], 1.0 / H)
 
-        def dummy(bank):
-            nc.tensor.matmul(out=bank[:, 0:P], lhsT=zf[:, :], rhs=zf[:, :], start=True, stop=True)
+        bias = keep.tile([P, PACK], F32, name="bias")
+        proj_bf = [keep.tile([P, PACK * J_HALF], BF16, name="proj_bf%d" % h, align_bytes=64) for h in range(2)]
+        sums = keep.tile([P, 2 * ROW_TILES], F32, name="sums")
+        first_part = keep.tile([P, ROW_TILES], F32, name="first_part")
+        unread = keep.tile([P, J_HALF], BF16, name="unread")
+        banks, grouped, quantised, proj_q = {}, {}, {}, {}
 
-        def bank_tile(n, name):
-            return psum.tile([P, 512], F32, name=name, tag="bank%d" % n)
+        taken = []
 
-        def transposes(x, k, n):
-            src, pair = srcs["%s%d" % (x, k)]
-            bank = bank_tile(n, "t%s%d" % (x, k))
-            s32 = src[:, :].bitcast(F32)
-            for q in range(4):
-                c0 = 512 * pair + 128 * q
-                nc.tensor.transpose(bank[:, 128 * q : 128 * (q + 1)], s32[:, c0 : c0 + 128], ident[:, :])
-            return bank
+        def next_bank(name):
+            taken.append(name)
+            return psum.tile([P, BANK], F32, name=name, tag="bank%d" % ((len(taken) - 1) % N_BANKS))
 
-        def copy_out(eng, bank, name):
-            g = keep.tile([P, 1024], BF16, name=name, align_bytes=64)
-            dst = g[:, :].bitcast(F32).rearrange("p (r c u) -> p r c u", r=2, u=2)
-            src = bank[:, :].rearrange("p (r u c) -> p r c u", r=2, u=2)
-            if eng == "v":
-                nc.vector.tensor_copy(out=dst, in_=src)
-            else:
+        idle_bank = psum.tile([P, BANK], F32, name="idle_bank", tag="bank%d" % (N_BANKS - 1))
+
+        def idle_matmuls(n):
+            for i in range(n):
+                nc.tensor.matmul(out=idle_bank[:, :], lhsT=zeros[:, 0:P], rhs=zeros[:, :], start=True, stop=True)
+
+        def transpose_pair(pair):
+            held, place = source[pair]
+            words = held[:, :].bitcast(F32)
+            banks[pair] = next_bank("t_" + pair)
+            for s in range(4):
+                c0 = BANK * place + P * s
+                nc.tensor.transpose(banks[pair][:, P * s : P * (s + 1)], words[:, c0 : c0 + P], ident[:, :])
+
+        def empty_pair(engine, pair):
+            grouped[pair] = keep.tile([P, 2 * P * PACK], BF16, name="g_" + pair, align_bytes=64)
+            dst = grouped[pair][:, :].bitcast(F32).rearrange("p (r c u) -> p r c u", r=2, u=2)
+            src = banks[pair][:, :].rearrange("p (r u c) -> p r c u", r=2, u=2)
+            if engine == "scalar":
                 nc.scalar.copy(out=dst, in_=src)
-            return g
+            else:
+                nc.vector.tensor_copy(out=dst, in_=src)
 
-        def quantise(g, width, name):
-            codes = keep.tile([P, width // 4], U32, name=name + "c", align_bytes=64)
-            scales = keep.tile([P, width // 4], U8, name=name + "s", align_bytes=64)
-            nc.vector.quantize_mx(out=codes[:, :].bitcast(FP8X4), scales=scales[:, :], in_=g[:, :])
-            return codes, scales
+        def quantise(name, values):
+            n_words = values.shape[1] // PACK
+            codes = keep.tile([P, n_words], U32, name="c_" + name, align_bytes=64)
+            plane = keep.tile([P, n_words], U8, name="s_" + name, align_bytes=64)
+            nc.vector.quantize_mx(out=codes[:, :].bitcast(FP8X4), scales=plane[:, :], in_=values[:, :])
+            return codes, plane
 
-        def cols(op, k):
-            codes, scales = op
-            return codes[:, 128 * k : 128 * (k + 1)].bitcast(FP8X4), scales[:, 128 * k : 128 * (k + 1)]
+        def quantise_pair(pair):
+            quantised[pair] = quantise(pair, grouped[pair])
 
-        def proj_mm(jc, n):
-            bank = bank_tile(n, "pj%d" % jc)
-            rhs, rhs_s = cols(qz["b%d" % (jc // 2)], jc % 2)
-            for t in range(4):
-                lhsT, lhsT_s = cols(qz["w%d" % (t // 2)], t % 2)
+        def row_tile(kind, n):
+            codes, plane = quantised["%s%d" % (kind, n // 2)]
+            cols = slice(P * (n % 2), P * (n % 2 + 1))
+            return codes[:, cols].bitcast(FP8X4), plane[:, cols]
+
+        def proj_passes(jt):
+            banks["p%d" % jt] = next_bank("p%d" % jt)
+            rhs, rhs_scale = row_tile("b", jt)
+            for t in range(PACK):
+                lhsT, lhsT_scale = row_tile("w", t)
                 nc.tensor.matmul_mx(
-                    out=bank[:, 128 * t : 128 * (t + 1)],
-                    lhsT=lhsT, lhsT_scale=lhsT_s, rhs=rhs, rhs_scale=rhs_s,
+                    out=banks["p%d" % jt][:, P * t : P * (t + 1)],
+                    lhsT=lhsT, lhsT_scale=lhsT_scale, rhs=rhs, rhs_scale=rhs_scale,
                     start=True, stop=True,
                 )
-            return bank
 
-        def proj_add(bank, c, k):
+        def add_bias(jt):
+            h, n = jt // 4, jt % 4
             nc.vector.tensor_tensor(
-                out=g2[c][:, 512 * k : 512 * (k + 1)].rearrange("p (j t) -> p j t", t=4),
-                in0=bank[:, :].rearrange("p (t j) -> p j t", t=4),
-                in1=bias_b,
+                out=proj_bf[h][:, BANK * n : BANK * (n + 1)].rearrange("p (j t) -> p j t", t=PACK),
+                in0=banks["p%d" % jt][:, :].rearrange("p (t j) -> p j t", t=PACK),
+                in1=bias[:, :].unsqueeze(1).to_broadcast([P, P, PACK]),
                 op=ALU.add,
             )
 
-        def score_mm(c, r, n):
-            bank = bank_tile(n, "sc%d_%d" % (c, r))
-            lhsT, lhsT_s = cols(qz["a%d" % (r // 2)], r % 2)
+        def quantise_proj(h):
+            proj_q[h] = quantise("proj%d" % h, proj_bf[h])
+
+        def scores_pass(h, r):
+            banks["s%d%d" % (h, r)] = next_bank("s%d%d" % (h, r))
+            lhsT, lhsT_scale = row_tile("a", r)
+            codes, plane = proj_q[h]
             nc.tensor.matmul_mx(
-                out=bank[:, 0 : WIDTHS[c]], lhsT=lhsT, lhsT_scale=lhsT_s,
-                rhs=pq[c][0][:, :].bitcast(FP8X4), rhs_scale=pq[c][1][:, :],
-                start=True, stop=True,
+                out=banks["s%d%d" % (h, r)][:, :], lhsT=lhsT, lhsT_scale=lhsT_scale,
+                rhs=codes[:, :].bitcast(FP8X4), rhs_scale=plane[:, :], start=True, stop=True,
             )
-            return bank
 
-        def score_sig(c, r):
+        def sigmoid_sum(h, r):
+            c = ROW_TILES * h + r
             nc.scalar.activation(
-                out=junk[:, 0 : WIDTHS[c]], in_=sc[(c, r)][:, 0 : WIDTHS[c]], func=ACT.Sigmoid,
-                accum_out=acc[:, 8 * c + r : 8 * c + r + 1],
+                out=unread[:, :], in_=banks["s%d%d" % (h, r)][:, :], func=ACT.Sigmoid, accum_out=sums[:, c : c + 1]
             )
 
-        def early_sums():
-            if NCH == 2:
-                nc.vector.tensor_scalar(out=acc0[:, :], in0=acc[:, 0:8], scalar1=1.0 / H, scalar2=None, op0=ALU.mult)
-            else:
-                nc.vector.tensor_tensor(out=acc0[:, :], in0=acc[:, 0:8], in1=acc[:, 8:16], op=ALU.add)
-                nc.vector.tensor_scalar(out=acc0[:, :], in0=acc0[:, :], scalar1=1.0 / H, scalar2=None, op0=ALU.mult)
-
-        def finish(r):
-            o_sb = outp.tile([P, H], F32, name="o_sb")
-            c = 8 * (NCH - 1) + r
+        def store_result(r):
+            res = results.tile([P, H], F32, name="res")
+            c = ROW_TILES + r
             nc.vector.tensor_scalar(
-                out=o_sb[:, :], in0=cdiv[:, :],
-                scalar1=acc[:, c : c + 1], scalar2=acc0[:, r : r + 1],
+                out=res[:, :], in0=inv_h[:, :], scalar1=sums[:, c : c + 1], scalar2=first_part[:, r : r + 1],
                 op0=ALU.mult, op1=ALU.add,
             )
-            nc.sync.dma_start(out=out_v[:, r, :], in_=o_sb[:, :])
+            nc.sync.dma_start(out=out_rows[:, r, :], in_=res[:, :])
 
-        dummy(dmy)
-        dummy(dmy)
-        dummy(dmy)
-        dummy(dmy)
-        dummy(dmy)
-        dummy(dmy)
-        tp["w0"] = transposes("w", 0, 0)
-        dummy(dmy)
-        tp["w1"] = transposes("w", 1, 1)
-        dummy(dmy)
-        gr["w0"] = copy_out("s", tp["w0"], "gw0")
-        tp["b0"] = transposes("b", 0, 2)
-        dummy(dmy)
-        gr["w1"] = copy_out("v", tp["w1"], "gw1")
-        tp["b1"] = transposes("b", 1, 3)
-        dummy(dmy)
-        dummy(dmy)
-        dummy(dmy)
-        qz["w0"] = quantise(gr["w0"], 1024, "qw0")
-        gr["b0"] = copy_out("s", tp["b0"], "gb0")
-        qz["w1"] = quantise(gr["w1"], 1024, "qw1")
-        gr["b1"] = copy_out("s", tp["b1"], "gb1")
-        qz["b0"] = quantise(gr["b0"], 1024, "qb0")
-        tp["a0"] = transposes("a", 0, 4)
-        qz["b1"] = quantise(gr["b1"], 1024, "qb1")
-        pj[0] = proj_mm(0, 5)
-        gr["a0"] = copy_out("s", tp["a0"], "ga0")
-        pj[1] = proj_mm(1, 6)
+        idle_matmuls(IDLE_FIRST)
+        transpose_pair("w0")
+        transpose_pair("w1")
+        idle_matmuls(1)
+        transpose_pair("b0")
+        transpose_pair("b1")
+        idle_matmuls(1)
+        transpose_pair("a0")
+        empty_pair("scalar", "w0")
+        empty_pair("vector", "w1")
+        quantise_pair("w0")
+        quantise_pair("w1")
+        for pair in ("b0", "b1"):
+            empty_pair("scalar", pair)
+            quantise_pair(pair)
+        empty_pair("scalar", "a0")
+
+        for jt in range(3):
+            proj_passes(jt)
         nc.vector.tensor_copy(out=bias[:, :], in_=b_bf[:, :])
-        proj_add(pj[0], 0, 0)
-        pj[2] = proj_mm(2, 7)
-        proj_add(pj[1], 0, 1)
-        tp["b2"] = transposes("b", 2, 0)
-        qz["a0"] = quantise(gr["a0"], 1024, "qa0")
-        proj_add(pj[2], 0, 2)
-        tp["b3"] = transposes("b", 3, 1)
-        late = bank_tile(2, "late0")
-        dummy(late)
-        gr["b2"] = copy_out("s", tp["b2"], "gb2")
-        pj[3] = proj_mm(3, 3)
-        gr["b3"] = copy_out("s", tp["b3"], "gb3")
-        qz["b2"] = quantise(gr["b2"], 1024, "qb2")
-        tp["a1"] = transposes("a", 1, 4)
-        proj_add(pj[3], 0, 3)
-        tp["a2"] = transposes("a", 2, 5)
-        gr["a1"] = copy_out("s", tp["a1"], "ga1")
-        tp["a3"] = transposes("a", 3, 6)
-        late = bank_tile(7, "late1")
-        dummy(late)
-        pq[0] = quantise(g2[0], 2048, "pq0")
-        pj[4] = proj_mm(4, 0)
-        gr["a2"] = copy_out("s", tp["a2"], "ga2")
-        pj[5] = proj_mm(5, 1)
-        qz["b3"] = quantise(gr["b3"], 1024, "qb3")
-        qz["a1"] = quantise(gr["a1"], 1024, "qa1")
-        sc[(0, 0)] = score_mm(0, 0, 2)
-        gr["a3"] = copy_out("s", tp["a3"], "ga3")
-        proj_add(pj[4], 1, 0)
-        sc[(0, 1)] = score_mm(0, 1, 3)
-        sc[(0, 2)] = score_mm(0, 2, 4)
-        score_sig(0, 0)
-        qz["a2"] = quantise(gr["a2"], 1024, "qa2")
-        sc[(0, 3)] = score_mm(0, 3, 5)
-        proj_add(pj[5], 1, 1)
-        pj[6] = proj_mm(6, 6)
-        score_sig(0, 1)
-        pj[7] = proj_mm(7, 7)
-        qz["a3"] = quantise(gr["a3"], 1024, "qa3")
-        sc[(0, 4)] = score_mm(0, 4, 0)
-        score_sig(0, 2)
-        proj_add(pj[6], 1, 2)
-        sc[(0, 5)] = score_mm(0, 5, 1)
-        score_sig(0, 3)
-        sc[(0, 6)] = score_mm(0, 6, 2)
-        proj_add(pj[7], 1, 3)
-        sc[(0, 7)] = score_mm(0, 7, 3)
-        score_sig(0, 4)
-        pq[1] = quantise(g2[1], 2048, "pq1")
-        score_sig(0, 5)
-        score_sig(0, 6)
-        sc[(1, 0)] = score_mm(1, 0, 4)
-        sc[(1, 1)] = score_mm(1, 1, 5)
-        sc[(1, 2)] = score_mm(1, 2, 6)
-        score_sig(0, 7)
-        sc[(1, 3)] = score_mm(1, 3, 7)
-        sc[(1, 4)] = score_mm(1, 4, 0)
-        score_sig(1, 0)
-        early_sums()
-        sc[(1, 5)] = score_mm(1, 5, 1)
-        sc[(1, 6)] = score_mm(1, 6, 2)
-        score_sig(1, 1)
-        finish(0)
-        sc[(1, 7)] = score_mm(1, 7, 3)
-        score_sig(1, 2)
-        finish(1)
-        score_sig(1, 3)
-        finish(2)
-        score_sig(1, 4)
-        finish(3)
-        score_sig(1, 5)
-        finish(4)
-        score_sig(1, 6)
-        finish(5)
-        score_sig(1, 7)
-        finish(6)
-        finish(7)
+        add_bias(0)
+        add_bias(1)
+        quantise_pair("a0")
+        add_bias(2)
+        for pair in ("b2", "b3"):
+            transpose_pair(pair)
+            empty_pair("scalar", pair)
+        proj_passes(3)
+        quantise_pair("b2")
+        add_bias(3)
+        quantise_proj(0)
+        for pair in ("a1", "a2", "a3"):
+            transpose_pair(pair)
+            empty_pair("scalar", pair)
+
+        quantise_pair("b3")
+        quantise_pair("a1")
+        proj_passes(4)
+        proj_passes(5)
+        for r in range(4):
+            scores_pass(0, r)
+        proj_passes(6)
+        proj_passes(7)
+        add_bias(4)
+        quantise_pair("a2")
+        add_bias(5)
+        quantise_pair("a3")
+        for r in range(4):
+            sigmoid_sum(0, r)
+        for r in range(4, ROW_TILES):
+            scores_pass(0, r)
+        add_bias(6)
+        add_bias(7)
+        quantise_proj(1)
+        for r in range(4, ROW_TILES):
+            sigmoid_sum(0, r)
+        nc.vector.tensor_scalar(
+            out=first_part[:, :], in0=sums[:, 0:ROW_TILES], scalar1=1.0 / H, scalar2=None, op0=ALU.mult
+        )
+
+        for r in range(ROW_TILES):
+            scores_pass(1, r)
+            sigmoid_sum(1, r)
+            store_result(r)

from contextlib import ExitStack

import concourse.mybir as mybir
from concourse.masks import make_identity

F32 = mybir.dt.float32
BF16 = mybir.dt.bfloat16
U32 = mybir.dt.uint32
U8 = mybir.dt.uint8
FP8X4 = mybir.dt.float8_e4m3fn_x4
ACT = mybir.ActivationFunctionType
ALU = mybir.AluOpType

P = 128
NA, NB, H = 1024, 1024, 512
FLOPS = 2 * NB * H * H + 2 * NA * NB * H
PACK = 4
BANK = 512
N_BANKS = 8
ROW_TILES = NA // P
J_HALF = NB // 2
IDLE_FIRST = 6


def tile_miscore_kernel(tc, y_a, y_b, W, b, out):
    nc = tc.nc
    with ExitStack() as ctx:
        keep = ctx.enter_context(tc.tile_pool(name="keep", bufs=1))
        results = ctx.enter_context(tc.tile_pool(name="results", bufs=4))
        psum = ctx.enter_context(tc.psum_pool(name="psum", bufs=1))
        ctx.enter_context(tc.manual_schedule())

        def load(name, n_tiles, rows):
            t = keep.tile([P, n_tiles * H], BF16, name=name)
            nc.sync.dma_start(out=t[:, :].rearrange("p (r k) -> p r k", r=n_tiles), in_=rows)
            return t

        ya_rows = y_a.rearrange("(p r) k -> p r k", r=ROW_TILES)
        out_rows = out.rearrange("(p r) k -> p r k", r=ROW_TILES)
        w_lo = load("w_lo", 2, W[0:256, :].rearrange("(p e) k -> p e k", e=2))
        w_hi = load("w_hi", 2, W[256:512, :].rearrange("(p e) k -> p e k", e=2))
        yb_0 = load("yb_0", 2, y_b[0:256, :].rearrange("(p r) k -> p r k", r=2))
        yb_1 = load("yb_1", 2, y_b[256:512, :].rearrange("(p r) k -> p r k", r=2))
        ya_lo = load("ya_lo", 4, ya_rows[:, 0:4, :])
        yb_hi = load("yb_hi", 4, y_b[512:1024, :].rearrange("(p r) k -> p r k", r=4))
        ya_hi = load("ya_hi", 4, ya_rows[:, 4:8, :])
        source = {
            "w0": (w_lo, 0), "w1": (w_hi, 0),
            "b0": (yb_0, 0), "b1": (yb_1, 0), "b2": (yb_hi, 0), "b3": (yb_hi, 1),
            "a0": (ya_lo, 0), "a1": (ya_lo, 1), "a2": (ya_hi, 0), "a3": (ya_hi, 1),
        }
        b_bf = keep.tile([P, PACK], BF16, name="b_bf")
        nc.scalar.dma_start(
            out=b_bf[:, :].rearrange("p (u e) -> p u e", u=2),
            in_=b.rearrange("(u p e) -> p u e", u=2, e=2),
        )

        zeros = keep.tile([P, BANK], BF16, name="zeros")
        nc.vector.memset(zeros[:, :], 0.0)
        one_col = keep.tile([P, 1], F32, name="one_col")
        one_sig = keep.tile([P, 1], F32, name="one_sig")
        nc.vector.memset(one_col[:, :], 0.0)
        nc.scalar.activation(out=one_sig[:, :], in_=one_col[:, :], func=ACT.Sigmoid)
        ident = keep.tile([P, P], F32, name="ident")
        make_identity(nc, ident[:, :])
        inv_h = keep.tile([P, H], F32, name="inv_h")
        nc.vector.memset(inv_h[:, :], 1.0 / H)

        bias = keep.tile([P, PACK], F32, name="bias")
        proj_bf = [keep.tile([P, PACK * J_HALF], BF16, name="proj_bf%d" % h, align_bytes=64) for h in range(2)]
        sums = keep.tile([P, 2 * ROW_TILES], F32, name="sums")
        first_part = keep.tile([P, ROW_TILES], F32, name="first_part")
        unread = keep.tile([P, J_HALF], BF16, name="unread")
        banks, grouped, quantised, proj_q = {}, {}, {}, {}

        taken = []

        def next_bank(name):
            taken.append(name)
            return psum.tile([P, BANK], F32, name=name, tag="bank%d" % ((len(taken) - 1) % N_BANKS))

        idle_bank = psum.tile([P, BANK], F32, name="idle_bank", tag="bank%d" % (N_BANKS - 1))

        def idle_matmuls(n):
            for i in range(n):
                nc.tensor.matmul(out=idle_bank[:, :], lhsT=zeros[:, 0:P], rhs=zeros[:, :], start=True, stop=True)

        def transpose_pair(pair):
            held, place = source[pair]
            words = held[:, :].bitcast(F32)
            banks[pair] = next_bank("t_" + pair)
            for s in range(4):
                c0 = BANK * place + P * s
                nc.tensor.transpose(banks[pair][:, P * s : P * (s + 1)], words[:, c0 : c0 + P], ident[:, :])

        def empty_pair(engine, pair):
            grouped[pair] = keep.tile([P, 2 * P * PACK], BF16, name="g_" + pair, align_bytes=64)
            dst = grouped[pair][:, :].bitcast(F32).rearrange("p (r c u) -> p r c u", r=2, u=2)
            src = banks[pair][:, :].rearrange("p (r u c) -> p r c u", r=2, u=2)
            if engine == "scalar":
                nc.scalar.copy(out=dst, in_=src)
            else:
                nc.vector.tensor_copy(out=dst, in_=src)

        def quantise(name, values):
            n_words = values.shape[1] // PACK
            codes = keep.tile([P, n_words], U32, name="c_" + name, align_bytes=64)
            plane = keep.tile([P, n_words], U8, name="s_" + name, align_bytes=64)
            nc.vector.quantize_mx(out=codes[:, :].bitcast(FP8X4), scales=plane[:, :], in_=values[:, :])
            return codes, plane

        def quantise_pair(pair):
            quantised[pair] = quantise(pair, grouped[pair])

        def row_tile(kind, n):
            codes, plane = quantised["%s%d" % (kind, n // 2)]
            cols = slice(P * (n % 2), P * (n % 2 + 1))
            return codes[:, cols].bitcast(FP8X4), plane[:, cols]

        def proj_passes(jt):
            banks["p%d" % jt] = next_bank("p%d" % jt)
            rhs, rhs_scale = row_tile("b", jt)
            for t in range(PACK):
                lhsT, lhsT_scale = row_tile("w", t)
                nc.tensor.matmul_mx(
                    out=banks["p%d" % jt][:, P * t : P * (t + 1)],
                    lhsT=lhsT, lhsT_scale=lhsT_scale, rhs=rhs, rhs_scale=rhs_scale,
                    start=True, stop=True,
                )

        def add_bias(jt):
            h, n = jt // 4, jt % 4
            nc.vector.tensor_tensor(
                out=proj_bf[h][:, BANK * n : BANK * (n + 1)].rearrange("p (j t) -> p j t", t=PACK),
                in0=banks["p%d" % jt][:, :].rearrange("p (t j) -> p j t", t=PACK),
                in1=bias[:, :].unsqueeze(1).to_broadcast([P, P, PACK]),
                op=ALU.add,
            )

        def quantise_proj(h):
            proj_q[h] = quantise("proj%d" % h, proj_bf[h])

        def scores_pass(h, r):
            banks["s%d%d" % (h, r)] = next_bank("s%d%d" % (h, r))
            lhsT, lhsT_scale = row_tile("a", r)
            codes, plane = proj_q[h]
            nc.tensor.matmul_mx(
                out=banks["s%d%d" % (h, r)][:, :], lhsT=lhsT, lhsT_scale=lhsT_scale,
                rhs=codes[:, :].bitcast(FP8X4), rhs_scale=plane[:, :], start=True, stop=True,
            )

        def sigmoid_sum(h, r):
            c = ROW_TILES * h + r
            nc.scalar.activation(
                out=unread[:, :], in_=banks["s%d%d" % (h, r)][:, :], func=ACT.Sigmoid, accum_out=sums[:, c : c + 1]
            )

        def store_result(r):
            res = results.tile([P, H], F32, name="res")
            c = ROW_TILES + r
            nc.vector.tensor_scalar(
                out=res[:, :], in0=inv_h[:, :], scalar1=sums[:, c : c + 1], scalar2=first_part[:, r : r + 1],
                op0=ALU.mult, op1=ALU.add,
            )
            nc.sync.dma_start(out=out_rows[:, r, :], in_=res[:, :])

        idle_matmuls(IDLE_FIRST)
        transpose_pair("w0")
        transpose_pair("w1")
        idle_matmuls(1)
        transpose_pair("b0")
        transpose_pair("b1")
        idle_matmuls(1)
        transpose_pair("a0")
        empty_pair("scalar", "w0")
        empty_pair("vector", "w1")
        quantise_pair("w0")
        quantise_pair("w1")
        for pair in ("b0", "b1"):
            empty_pair("scalar", pair)
            quantise_pair(pair)
        empty_pair("scalar", "a0")

        for jt in range(3):
            proj_passes(jt)
        nc.vector.tensor_copy(out=bias[:, :], in_=b_bf[:, :])
        add_bias(0)
        add_bias(1)
        quantise_pair("a0")
        add_bias(2)
        for pair in ("b2", "b3"):
            transpose_pair(pair)
            empty_pair("scalar", pair)
        proj_passes(3)
        quantise_pair("b2")
        add_bias(3)
        quantise_proj(0)
        for pair in ("a1", "a2", "a3"):
            transpose_pair(pair)
            empty_pair("scalar", pair)

        quantise_pair("b3")
        quantise_pair("a1")
        proj_passes(4)
        proj_passes(5)
        for r in range(4):
            scores_pass(0, r)
        proj_passes(6)
        proj_passes(7)
        add_bias(4)
        quantise_pair("a2")
        add_bias(5)
        quantise_pair("a3")
        for r in range(4):
            sigmoid_sum(0, r)
        for r in range(4, ROW_TILES):
            scores_pass(0, r)
        add_bias(6)
        add_bias(7)
        quantise_proj(1)
        for r in range(4, ROW_TILES):
            sigmoid_sum(0, r)
        nc.vector.tensor_scalar(
            out=first_part[:, :], in0=sums[:, 0:ROW_TILES], scalar1=1.0 / H, scalar2=None, op0=ALU.mult
        )

        for r in range(ROW_TILES):
            scores_pass(1, r)
            sigmoid_sum(1, r)
            store_result(r)
